import numpy as np
import ml_dtypes


def mxq(x, axis, fmt="e4m3"):
    dtype, down = {"e4m3": (ml_dtypes.float8_e4m3fn, 7), "e5m2": (ml_dtypes.float8_e5m2, 14)}[fmt]
    v = np.moveaxis(np.asarray(x, np.float32).astype(ml_dtypes.bfloat16).astype(np.float64), axis, -1)
    blocks = v.reshape(v.shape[:-1] + (-1, 32))
    amax = np.abs(blocks).max(-1, keepdims=True)
    byte = np.maximum(np.where(amax > 0, np.frexp(amax)[1] - 1 + 127, 0) - down, 1)
    scale = np.exp2(byte - 127.0)
    codes = (blocks / scale).astype(np.float32).astype(dtype).astype(np.float64)
    return np.moveaxis((codes * scale).reshape(v.shape), -1, axis)


WIDE = False


def mx_kscale(k):
    if not WIDE:
        return np.ones(k)
    levels = np.array([10, -10, 5, -5, 0])
    a = np.random.permutation(np.resize(levels, k // 512 * 4)).reshape(k // 512, 4)
    idx = np.arange(k)
    return np.exp2(a[idx // 512, idx % 128 // 32])


BF16 = ml_dtypes.bfloat16


def bf(x):
    return np.asarray(x, np.float32).astype(BF16)


def f64(x):
    return np.asarray(x).astype(np.float64)


B, E, D = 4096, 512, 256


def setup_inputs():
    s = mx_kscale(E)
    ws = 1.0 / np.sqrt(E)
    return {
        "x": bf(np.random.standard_normal((B, E)) * s),
        "state_A": bf(np.random.uniform(0.0, 1.0, (B, D))),
        "state_B": bf(0.5 + np.random.uniform(0.0, 1.0, (B, D))),
        "state_p": bf(np.random.standard_normal((B, D))),
        "state_x": bf(np.random.standard_normal((B, E)) * s),
        "time_decay": bf(0.5 * np.random.standard_normal(D)),
        "time_first": bf(np.log(0.3) + 0.3 * np.random.standard_normal(D)),
        "time_mix_k": bf(np.random.uniform(0.0, 1.0, (1, E))),
        "time_mix_v": bf(np.random.uniform(0.0, 1.0, (1, E))),
        "W_key": bf(np.random.standard_normal((D, E)) * ws / s[None, :]),
        "W_value": bf(np.random.standard_normal((D, E)) * ws / s[None, :]),
    }


def reference(x, state_A, state_B, state_p, state_x, time_decay, time_first, time_mix_k, time_mix_v, W_key, W_value):
    x, state_x = f64(x), f64(state_x)
    state_A, state_B, state_p = f64(state_A), f64(state_B), f64(state_p)
    mk, mv = f64(time_mix_k), f64(time_mix_v)
    xk = x * mk + state_x * (1.0 - mk)
    xv = x * mv + state_x * (1.0 - mv)
    k = mxq(xk, 1, "e4m3") @ mxq(f64(W_key), 1, "e4m3").T
    v = mxq(xv, 1, "e4m3") @ mxq(f64(W_value), 1, "e4m3").T
    ww = f64(time_first) + k
    p = np.maximum(state_p, ww)
    e1 = np.exp(state_p - p)
    e2 = np.exp(ww - p)
    a = e1 * state_A + e2 * v
    b = e1 * state_B + e2
    td = -np.exp(f64(time_decay))
    ww = state_p + td
    p = np.maximum(ww, k)
    e1 = np.exp(ww - p)
    e2 = np.exp(k - p)
    new_A = e1 * state_A + e2 * v
    new_B = e1 * state_B + e2
    return (a, b, new_A, new_B, p)

@@ -1,0 +1,177 @@
+from contextlib import ExitStack
+
+import concourse.mybir as mybir
+from concourse.masks import make_identity
+
+F32 = mybir.dt.float32
+BF16 = mybir.dt.bfloat16
+U32 = mybir.dt.uint32
+U8 = mybir.dt.uint8
+FP8X4 = mybir.dt.float8_e4m3fn_x4
+ALU = mybir.AluOpType
+ACT = mybir.ActivationFunctionType
+
+P = 128
+B = 4096
+E = 512
+D = 256
+NJ = B // P
+PACK = 4
+JB = 4
+NB = NJ // JB
+FLOPS = 2 * B * E * D * 2
+
+
+def tile_rwkv_timemix_for_quant_pa_t_kernel(
+    tc, x, state_A, state_B, state_p, state_x, time_decay, time_first,
+    time_mix_k, time_mix_v, W_key, W_value, out_0, out_1, out_2, out_3, out_4,
+):
+    nc = tc.nc
+    with ExitStack() as ctx:
+        const = ctx.enter_context(tc.tile_pool(name="const", bufs=1))
+        loads = ctx.enter_context(tc.tile_pool(name="loads", bufs=3))
+        work = ctx.enter_context(tc.tile_pool(name="work", bufs=2))
+        outs = ctx.enter_context(tc.tile_pool(name="outs", bufs=2))
+        psum = ctx.enter_context(tc.psum_pool(name="psum", bufs=1))
+
+        x_v = x.rearrange("(p j) k -> p j k", j=NJ)
+        sx_v = state_x.rearrange("(p j) k -> p j k", j=NJ)
+        sa_v = state_A.rearrange("(p j) d -> p j d", j=NJ)
+        sb_v = state_B.rearrange("(p j) d -> p j d", j=NJ)
+        sp_v = state_p.rearrange("(p j) d -> p j d", j=NJ)
+        out_v = [o.rearrange("(p j) d -> p j d", j=NJ) for o in (out_0, out_1, out_2, out_3, out_4)]
+
+        ident = const.tile([P, P], BF16, name="ident")
+        make_identity(nc, ident[:])
+
+        vecs = const.tile([P, P], BF16, name="vecs")
+        nc.vector.memset(vecs[:], 0.0)
+        nc.sync.dma_start(out=vecs[0:4, :], in_=time_mix_k.rearrange("o (t p) -> (o t) p", p=P))
+        nc.sync.dma_start(out=vecs[4:8, :], in_=time_mix_v.rearrange("o (t p) -> (o t) p", p=P))
+        w_sb = []
+        for wi, w in enumerate((W_key, W_value)):
+            wt = const.tile([P, 2, E], BF16, name="w_sb%d" % wi)
+            nc.sync.dma_start(out=wt[:], in_=w.rearrange("(h p) k -> p h k", p=P))
+            w_sb.append(wt)
+        tf_bf = const.tile([P, D], BF16, name="tf_bf")
+        nc.sync.dma_start(out=tf_bf[:], in_=time_first.partition_broadcast(P))
+        td_bf = const.tile([P, D], BF16, name="td_bf")
+        nc.sync.dma_start(out=td_bf[:], in_=time_decay.partition_broadcast(P))
+
+        vecs_t = psum.tile([P, P], BF16, name="vecs_t", tag="xT0")
+        nc.tensor.transpose(vecs_t[:], vecs[:], ident[:])
+        mix = const.tile([P, 8], F32, name="mix")
+        nc.vector.tensor_copy(out=mix[:], in_=vecs_t[:, 0:8])
+        omix = const.tile([P, 8], F32, name="omix")
+        nc.vector.tensor_scalar(out=omix[:], in0=mix[:], scalar1=-1.0, scalar2=1.0, op0=ALU.mult, op1=ALU.add)
+
+        tf4 = const.tile([P, JB, D], F32, name="tf4")
+        ed4 = const.tile([P, JB, D], F32, name="ed4")
+        for jj in range(JB):
+            nc.vector.tensor_copy(out=tf4[:, jj, :], in_=tf_bf[:])
+            nc.scalar.activation(out=ed4[:, jj, :], in_=td_bf[:], func=ACT.Exp)
+
+        w_codes = []
+        w_scales = []
+        for wi in range(2):
+            w_t = psum.tile([P, PACK, D], BF16, name="w_t%d" % wi, tag="sxT%d" % wi)
+            for h in range(2):
+                for t in range(PACK):
+                    nc.tensor.transpose(w_t[:, t, h * P:(h + 1) * P], w_sb[wi][:, h, t * P:(t + 1) * P], ident[:])
+            wg = const.tile([P, D, PACK], BF16, name="wg%d" % wi, align_bytes=64)
+            nc.vector.tensor_copy(out=wg[:], in_=w_t[:].rearrange("p t d -> p d t"))
+            wc = const.tile([P, D], U32, name="wc%d" % wi, align_bytes=64)
+            ws = const.tile([P, D], U8, name="ws%d" % wi, align_bytes=64)
+            nc.vector.quantize_mx(out=wc[:].bitcast(FP8X4), scales=ws[:], in_=wg[:].rearrange("p d t -> p (d t)"))
+            w_codes.append(wc)
+            w_scales.append(ws)
+
+        R = JB * P
+        for b in range(NB):
+            js = slice(b * JB, (b + 1) * JB)
+            x_sb = loads.tile([P, JB, E], BF16, name="x_sb")
+            nc.sync.dma_start(out=x_sb[:], in_=x_v[:, js, :])
+            sx_sb = loads.tile([P, JB, E], BF16, name="sx_sb")
+            nc.sync.dma_start(out=sx_sb[:], in_=sx_v[:, js, :])
+            sp_sb = loads.tile([P, JB, D], BF16, name="sp_sb")
+            nc.sync.dma_start(out=sp_sb[:], in_=sp_v[:, js, :])
+            sa_sb = loads.tile([P, JB, D], BF16, name="sa_sb")
+            nc.sync.dma_start(out=sa_sb[:], in_=sa_v[:, js, :])
+            sb_sb = loads.tile([P, JB, D], BF16, name="sb_sb")
+            nc.sync.dma_start(out=sb_sb[:], in_=sb_v[:, js, :])
+
+            q1 = work.tile([P, JB, D], F32, name="q1")
+            nc.gpsimd.tensor_tensor(out=q1[:], in0=sp_sb[:], in1=tf4[:], op=ALU.subtract)
+            q2 = work.tile([P, JB, D], F32, name="q2")
+            nc.gpsimd.tensor_tensor(out=q2[:], in0=sp_sb[:], in1=ed4[:], op=ALU.subtract)
+
+            planes = [work.tile([P, PACK, R], BF16, name="plane%d" % m) for m in range(2)]
+            for hf in range(2):
+                xT = psum.tile([P, 2, R], BF16, name="xT", tag="xT%d" % hf)
+                sxT = psum.tile([P, 2, R], BF16, name="sxT", tag="sxT%d" % hf)
+                for tt in range(2):
+                    t = 2 * hf + tt
+                    for jj in range(JB):
+                        nc.tensor.transpose(sxT[:, tt, jj * P:(jj + 1) * P], sx_sb[:, jj, t * P:(t + 1) * P], ident[:])
+                for tt in range(2):
+                    t = 2 * hf + tt
+                    for jj in range(JB):
+                        nc.tensor.transpose(xT[:, tt, jj * P:(jj + 1) * P], x_sb[:, jj, t * P:(t + 1) * P], ident[:])
+                for m in range(2):
+                    u = work.tile([P, 2, R], F32, name="u%d" % m)
+                    for tt in range(2):
+                        t = 2 * hf + tt
+                        c = 4 * m + t
+                        nc.scalar.activation(out=u[:, tt, :], in_=sxT[:, tt, :], func=ACT.Copy, scale=omix[:, c:c + 1])
+                        nc.vector.scalar_tensor_tensor(
+                            out=planes[m][:, t, :], in0=xT[:, tt, :], scalar=mix[:, c:c + 1], in1=u[:, tt, :],
+                            op0=ALU.mult, op1=ALU.add)
+
+            codes = []
+            scales = []
+            for m in range(2):
+                grouped = work.tile([P, R, PACK], BF16, name="grouped%d" % m, align_bytes=64)
+                nc.scalar.copy(
+                    out=grouped[:].rearrange("p (c i) t -> p c t i", i=4),
+                    in_=planes[m][:].rearrange("p t (c i) -> p c t i", i=4))
+                cd = work.tile([P, R], U32, name="cd%d" % m, align_bytes=64)
+                sc = work.tile([P, R], U8, name="sc%d" % m, align_bytes=64)
+                nc.vector.quantize_mx(out=cd[:].bitcast(FP8X4), scales=sc[:], in_=grouped[:].rearrange("p r t -> p (r t)"))
+                codes.append(cd)
+                scales.append(sc)
+
+            o_t = [outs.tile([P, JB, D], F32, name="o%d" % i) for i in range(5)]
+            for pr in range(JB // 2):
+                kv = []
+                for m in range(2):
+                    acc = psum.tile([P, 2, D], F32, name="acc%d" % m, bufs=2)
+                    for j2 in range(2):
+                        jj = 2 * pr + j2
+                        cols = slice(jj * P, (jj + 1) * P)
+                        nc.tensor.matmul_mx(
+                            out=acc[:, j2, :], lhsT=codes[m][:, cols].bitcast(FP8X4), lhsT_scale=scales[m][:, cols],
+                            rhs=w_codes[m][:].bitcast(FP8X4), rhs_scale=w_scales[m][:], start=True, stop=True)
+                    kv.append(acc)
+                k_ps, v_ps = kv
+                ps = slice(2 * pr, 2 * pr + 2)
+                sa = sa_sb[:, ps, :]
+                sb = sb_sb[:, ps, :]
+                nc.vector.tensor_tensor(out=o_t[4][:, ps, :], in0=q2[:, ps, :], in1=k_ps[:], op=ALU.max)
+                for half, q in enumerate((q1, q2)):
+                    dl = work.tile([P, 2, D], F32, name="dl%d" % half)
+                    nc.vector.tensor_tensor(out=dl[:], in0=q[:, ps, :], in1=k_ps[:], op=ALU.subtract)
+                    ep = work.tile([P, 2, D], F32, name="ep%d" % half)
+                    nc.scalar.activation(out=ep[:], in_=dl[:], func=ACT.Exp)
+                    em = work.tile([P, 2, D], F32, name="em%d" % half)
+                    nc.scalar.activation(out=em[:], in_=dl[:], func=ACT.Exp, scale=-1.0)
+                    t1 = work.tile([P, 2, D], F32, name="t1_%d" % half)
+                    nc.vector.scalar_tensor_tensor(out=t1[:], in0=ep[:], scalar=1.0, in1=sa, op0=ALU.min, op1=ALU.mult)
+                    t3 = work.tile([P, 2, D], F32, name="t3_%d" % half)
+                    nc.vector.scalar_tensor_tensor(out=t3[:], in0=ep[:], scalar=1.0, in1=sb, op0=ALU.min, op1=ALU.mult)
+                    t2 = work.tile([P, 2, D], F32, name="t2_%d" % half)
+                    nc.vector.scalar_tensor_tensor(out=t2[:], in0=em[:], scalar=1.0, in1=v_ps[:], op0=ALU.min, op1=ALU.mult)
+                    nc.vector.scalar_tensor_tensor(
+                        out=o_t[2 * half + 1][:, ps, :], in0=em[:], scalar=1.0, in1=t3[:], op0=ALU.min, op1=ALU.add)
+                    nc.gpsimd.tensor_tensor(out=o_t[2 * half][:, ps, :], in0=t1[:], in1=t2[:], op=ALU.add)
+            for i in range(5):
+                nc.sync.dma_start(out=out_v[i][:, js, :], in_=o_t[i][:])

@@ -101,9 +101,9 @@ def tile_rwkv_timemix_for_quant_pa_t_kernel(
             nc.sync.dma_start(out=sb_sb[:], in_=sb_v[:, js, :])
 
             q1 = work.tile([P, JB, D], F32, name="q1")
-            nc.gpsimd.tensor_tensor(out=q1[:], in0=sp_sb[:], in1=tf4[:], op=ALU.subtract)
+            nc.vector.tensor_tensor(out=q1[:], in0=sp_sb[:], in1=tf4[:], op=ALU.subtract)
             q2 = work.tile([P, JB, D], F32, name="q2")
-            nc.gpsimd.tensor_tensor(out=q2[:], in0=sp_sb[:], in1=ed4[:], op=ALU.subtract)
+            nc.vector.tensor_tensor(out=q2[:], in0=sp_sb[:], in1=ed4[:], op=ALU.subtract)
 
             planes = [work.tile([P, PACK, R], BF16, name="plane%d" % m) for m in range(2)]
             for hf in range(2):
@@ -172,6 +172,6 @@ def tile_rwkv_timemix_for_quant_pa_t_kernel(
                     nc.vector.scalar_tensor_tensor(out=t2[:], in0=em[:], scalar=1.0, in1=v_ps[:], op0=ALU.min, op1=ALU.mult)
                     nc.vector.scalar_tensor_tensor(
                         out=o_t[2 * half + 1][:, ps, :], in0=em[:], scalar=1.0, in1=t3[:], op0=ALU.min, op1=ALU.add)
-                    nc.gpsimd.tensor_tensor(out=o_t[2 * half][:, ps, :], in0=t1[:], in1=t2[:], op=ALU.add)
+                    nc.vector.tensor_tensor(out=o_t[2 * half][:, ps, :], in0=t1[:], in1=t2[:], op=ALU.add)
             for i in range(5):
                 nc.sync.dma_start(out=out_v[i][:, js, :], in_=o_t[i][:])

@@ -19,7 +19,10 @@ NJ = B // P
 PACK = 4
 JB = 4
 NB = NJ // JB
+R = JB * P
+NH = D // P
 FLOPS = 2 * B * E * D * 2
+VECTOR_EVACS = ()
 
 
 def tile_rwkv_timemix_for_quant_pa_t_kernel(
@@ -43,39 +46,42 @@ def tile_rwkv_timemix_for_quant_pa_t_kernel(
 
         ident = const.tile([P, P], BF16, name="ident")
         make_identity(nc, ident[:])
+        ident32 = const.tile([P, P], F32, name="ident32")
+        make_identity(nc, ident32[:])
 
         vecs = const.tile([P, P], BF16, name="vecs")
         nc.vector.memset(vecs[:], 0.0)
         nc.sync.dma_start(out=vecs[0:4, :], in_=time_mix_k.rearrange("o (t p) -> (o t) p", p=P))
         nc.sync.dma_start(out=vecs[4:8, :], in_=time_mix_v.rearrange("o (t p) -> (o t) p", p=P))
+        nc.sync.dma_start(out=vecs[8:10, :], in_=time_first.rearrange("(h p) -> h p", p=P))
+        nc.sync.dma_start(out=vecs[10:12, :], in_=time_decay.rearrange("(h p) -> h p", p=P))
         w_sb = []
         for wi, w in enumerate((W_key, W_value)):
-            wt = const.tile([P, 2, E], BF16, name="w_sb%d" % wi)
+            wt = const.tile([P, NH, E], BF16, name="w_sb%d" % wi)
             nc.sync.dma_start(out=wt[:], in_=w.rearrange("(h p) k -> p h k", p=P))
             w_sb.append(wt)
-        tf_bf = const.tile([P, D], BF16, name="tf_bf")
-        nc.sync.dma_start(out=tf_bf[:], in_=time_first.partition_broadcast(P))
-        td_bf = const.tile([P, D], BF16, name="td_bf")
-        nc.sync.dma_start(out=td_bf[:], in_=time_decay.partition_broadcast(P))
 
-        vecs_t = psum.tile([P, P], BF16, name="vecs_t", tag="xT0")
+        vecs_t = psum.tile([P, P], BF16, name="vecs_t", tag="xT")
         nc.tensor.transpose(vecs_t[:], vecs[:], ident[:])
-        mix = const.tile([P, 8], F32, name="mix")
-        nc.vector.tensor_copy(out=mix[:], in_=vecs_t[:, 0:8])
+        cst = const.tile([P, 12], F32, name="cst")
+        nc.vector.tensor_copy(out=cst[:], in_=vecs_t[:, 0:12])
+        mix = cst[:, 0:8]
         omix = const.tile([P, 8], F32, name="omix")
-        nc.vector.tensor_scalar(out=omix[:], in0=mix[:], scalar1=-1.0, scalar2=1.0, op0=ALU.mult, op1=ALU.add)
-
-        tf4 = const.tile([P, JB, D], F32, name="tf4")
-        ed4 = const.tile([P, JB, D], F32, name="ed4")
-        for jj in range(JB):
-            nc.vector.tensor_copy(out=tf4[:, jj, :], in_=tf_bf[:])
-            nc.scalar.activation(out=ed4[:, jj, :], in_=td_bf[:], func=ACT.Exp)
+        nc.vector.tensor_scalar(out=omix[:], in0=mix, scalar1=-1.0, scalar2=1.0, op0=ALU.mult, op1=ALU.add)
+        ed = const.tile([P, NH], F32, name="ed")
+        nc.scalar.activation(out=ed[:], in_=cst[:, 10:12], func=ACT.Exp)
+        td = const.tile([P, NH], F32, name="td")
+        nc.vector.tensor_scalar(out=td[:], in0=ed[:], scalar1=-1.0, scalar2=None, op0=ALU.mult)
+        c1 = const.tile([P, NH], F32, name="c1")
+        nc.vector.tensor_tensor(out=c1[:], in0=ed[:], in1=cst[:, 8:10], op=ALU.subtract)
+        nc1 = const.tile([P, NH], F32, name="nc1")
+        nc.vector.tensor_scalar(out=nc1[:], in0=c1[:], scalar1=-1.0, scalar2=None, op0=ALU.mult)
 
         w_codes = []
         w_scales = []
         for wi in range(2):
-            w_t = psum.tile([P, PACK, D], BF16, name="w_t%d" % wi, tag="sxT%d" % wi)
-            for h in range(2):
+            w_t = psum.tile([P, PACK, D], BF16, name="w_t%d" % wi, tag="sxT", bufs=2)
+            for h in range(NH):
                 for t in range(PACK):
                     nc.tensor.transpose(w_t[:, t, h * P:(h + 1) * P], w_sb[wi][:, h, t * P:(t + 1) * P], ident[:])
             wg = const.tile([P, D, PACK], BF16, name="wg%d" % wi, align_bytes=64)
@@ -86,7 +92,6 @@ def tile_rwkv_timemix_for_quant_pa_t_kernel(
             w_codes.append(wc)
             w_scales.append(ws)
 
-        R = JB * P
         for b in range(NB):
             js = slice(b * JB, (b + 1) * JB)
             x_sb = loads.tile([P, JB, E], BF16, name="x_sb")
@@ -100,15 +105,10 @@ def tile_rwkv_timemix_for_quant_pa_t_kernel(
             sb_sb = loads.tile([P, JB, D], BF16, name="sb_sb")
             nc.sync.dma_start(out=sb_sb[:], in_=sb_v[:, js, :])
 
-            q1 = work.tile([P, JB, D], F32, name="q1")
-            nc.vector.tensor_tensor(out=q1[:], in0=sp_sb[:], in1=tf4[:], op=ALU.subtract)
-            q2 = work.tile([P, JB, D], F32, name="q2")
-            nc.vector.tensor_tensor(out=q2[:], in0=sp_sb[:], in1=ed4[:], op=ALU.subtract)
-
             planes = [work.tile([P, PACK, R], BF16, name="plane%d" % m) for m in range(2)]
             for hf in range(2):
-                xT = psum.tile([P, 2, R], BF16, name="xT", tag="xT%d" % hf)
-                sxT = psum.tile([P, 2, R], BF16, name="sxT", tag="sxT%d" % hf)
+                sxT = psum.tile([P, 2, R], BF16, name="sxT", tag="sxT", bufs=2)
+                xT = psum.tile([P, 2, R], BF16, name="xT", tag="xT")
                 for tt in range(2):
                     t = 2 * hf + tt
                     for jj in range(JB):
@@ -124,54 +124,83 @@ def tile_rwkv_timemix_for_quant_pa_t_kernel(
                         c = 4 * m + t
                         nc.scalar.activation(out=u[:, tt, :], in_=sxT[:, tt, :], func=ACT.Copy, scale=omix[:, c:c + 1])
                         nc.vector.scalar_tensor_tensor(
-                            out=planes[m][:, t, :], in0=xT[:, tt, :], scalar=mix[:, c:c + 1], in1=u[:, tt, :],
+                            out=planes[m][:, t, :], in0=xT[:, tt, :], scalar=cst[:, c:c + 1], in1=u[:, tt, :],
                             op0=ALU.mult, op1=ALU.add)
 
             codes = []
             scales = []
             for m in range(2):
                 grouped = work.tile([P, R, PACK], BF16, name="grouped%d" % m, align_bytes=64)
-                nc.scalar.copy(
+                nc.vector.tensor_copy(
                     out=grouped[:].rearrange("p (c i) t -> p c t i", i=4),
                     in_=planes[m][:].rearrange("p t (c i) -> p c t i", i=4))
-                cd = work.tile([P, R], U32, name="cd%d" % m, align_bytes=64)
-                sc = work.tile([P, R], U8, name="sc%d" % m, align_bytes=64)
-                nc.vector.quantize_mx(out=cd[:].bitcast(FP8X4), scales=sc[:], in_=grouped[:].rearrange("p r t -> p (r t)"))
-                codes.append(cd)
-                scales.append(sc)
+                codes.append(work.tile([P, R], U32, name="cd%d" % m, align_bytes=64))
+                scales.append(work.tile([P, R], U8, name="sc%d" % m, align_bytes=64))
+                nc.vector.quantize_mx(
+                    out=codes[m][:].bitcast(FP8X4), scales=scales[m][:], in_=grouped[:].rearrange("p r t -> p (r t)"))
+
+            spT = psum.tile([P, NH, R], BF16, name="spT", tag="sxT", bufs=2)
+            for h in range(NH):
+                for jj in range(JB):
+                    nc.tensor.transpose(spT[:, h, jj * P:(jj + 1) * P], sp_sb[:, jj, h * P:(h + 1) * P], ident[:])
+            q2 = work.tile([P, NH, R], F32, name="q2")
+            for h in range(NH):
+                nc.scalar.activation(out=q2[:, h, :], in_=spT[:, h, :], func=ACT.Identity, bias=td[:, h:h + 1])
 
             o_t = [outs.tile([P, JB, D], F32, name="o%d" % i) for i in range(5)]
-            for pr in range(JB // 2):
+            for h in range(NH):
+                hs = slice(h * P, (h + 1) * P)
+                sabT = psum.tile([P, 2, R], BF16, name="sabT")
+                for si, s_sb in enumerate((sa_sb, sb_sb)):
+                    for jj in range(JB):
+                        nc.tensor.transpose(sabT[:, si, jj * P:(jj + 1) * P], s_sb[:, jj, hs], ident[:])
                 kv = []
                 for m in range(2):
-                    acc = psum.tile([P, 2, D], F32, name="acc%d" % m, bufs=2)
-                    for j2 in range(2):
-                        jj = 2 * pr + j2
-                        cols = slice(jj * P, (jj + 1) * P)
-                        nc.tensor.matmul_mx(
-                            out=acc[:, j2, :], lhsT=codes[m][:, cols].bitcast(FP8X4), lhsT_scale=scales[m][:, cols],
-                            rhs=w_codes[m][:].bitcast(FP8X4), rhs_scale=w_scales[m][:], start=True, stop=True)
+                    acc = psum.tile([P, R], F32, name="acc%d" % m)
+                    nc.tensor.matmul_mx(
+                        out=acc[:], lhsT=w_codes[m][:, hs].bitcast(FP8X4), lhsT_scale=w_scales[m][:, hs],
+                        rhs=codes[m][:].bitcast(FP8X4), rhs_scale=scales[m][:], start=True, stop=True)
                     kv.append(acc)
                 k_ps, v_ps = kv
-                ps = slice(2 * pr, 2 * pr + 2)
-                sa = sa_sb[:, ps, :]
-                sb = sb_sb[:, ps, :]
-                nc.vector.tensor_tensor(out=o_t[4][:, ps, :], in0=q2[:, ps, :], in1=k_ps[:], op=ALU.max)
-                for half, q in enumerate((q1, q2)):
-                    dl = work.tile([P, 2, D], F32, name="dl%d" % half)
-                    nc.vector.tensor_tensor(out=dl[:], in0=q[:, ps, :], in1=k_ps[:], op=ALU.subtract)
-                    ep = work.tile([P, 2, D], F32, name="ep%d" % half)
-                    nc.scalar.activation(out=ep[:], in_=dl[:], func=ACT.Exp)
-                    em = work.tile([P, 2, D], F32, name="em%d" % half)
-                    nc.scalar.activation(out=em[:], in_=dl[:], func=ACT.Exp, scale=-1.0)
-                    t1 = work.tile([P, 2, D], F32, name="t1_%d" % half)
-                    nc.vector.scalar_tensor_tensor(out=t1[:], in0=ep[:], scalar=1.0, in1=sa, op0=ALU.min, op1=ALU.mult)
-                    t3 = work.tile([P, 2, D], F32, name="t3_%d" % half)
-                    nc.vector.scalar_tensor_tensor(out=t3[:], in0=ep[:], scalar=1.0, in1=sb, op0=ALU.min, op1=ALU.mult)
-                    t2 = work.tile([P, 2, D], F32, name="t2_%d" % half)
-                    nc.vector.scalar_tensor_tensor(out=t2[:], in0=em[:], scalar=1.0, in1=v_ps[:], op0=ALU.min, op1=ALU.mult)
+                d2 = work.tile([P, R], F32, name="d2")
+                nc.vector.tensor_tensor(out=d2[:], in0=q2[:, h, :], in1=k_ps[:], op=ALU.subtract)
+                r2 = work.tile([P, R], F32, name="r2")
+                nc.scalar.activation(out=r2[:], in_=d2[:], func=ACT.Relu, scale=-1.0)
+                pairs = [None, None, None, None, (q2[:, h, :], r2[:])]
+                for half in range(2):
+                    ep = work.tile([P, R], F32, name="ep%d" % half)
+                    em = work.tile([P, R], F32, name="em%d" % half)
+                    if half == 0:
+                        nc.scalar.activation(out=ep[:], in_=d2[:], func=ACT.Exp, bias=c1[:, h:h + 1])
+                        nc.scalar.activation(out=em[:], in_=d2[:], func=ACT.Exp, bias=nc1[:, h:h + 1], scale=-1.0)
+                    else:
+                        nc.scalar.activation(out=ep[:], in_=d2[:], func=ACT.Exp)
+                        nc.scalar.activation(out=em[:], in_=d2[:], func=ACT.Exp, scale=-1.0)
+                    t1 = work.tile([P, R], F32, name="t1_%d" % half)
                     nc.vector.scalar_tensor_tensor(
-                        out=o_t[2 * half + 1][:, ps, :], in0=em[:], scalar=1.0, in1=t3[:], op0=ALU.min, op1=ALU.add)
-                    nc.vector.tensor_tensor(out=o_t[2 * half][:, ps, :], in0=t1[:], in1=t2[:], op=ALU.add)
+                        out=t1[:], in0=ep[:], scalar=1.0, in1=sabT[:, 0, :], op0=ALU.min, op1=ALU.mult)
+                    t3 = work.tile([P, R], F32, name="t3_%d" % half)
+                    nc.vector.scalar_tensor_tensor(
+                        out=t3[:], in0=ep[:], scalar=1.0, in1=sabT[:, 1, :], op0=ALU.min, op1=ALU.mult)
+                    t2 = work.tile([P, R], F32, name="t2_%d" % half)
+                    nc.vector.scalar_tensor_tensor(
+                        out=t2[:], in0=em[:], scalar=1.0, in1=v_ps[:], op0=ALU.min, op1=ALU.mult)
+                    e2 = work.tile([P, R], F32, name="e2_%d" % half)
+                    nc.vector.tensor_scalar(out=e2[:], in0=em[:], scalar1=1.0, scalar2=None, op0=ALU.min)
+                    pairs[2 * half] = (t1[:], t2[:])
+                    pairs[2 * half + 1] = (t3[:], e2[:])
+                for i in (4, 0, 1, 2, 3):
+                    first, second = pairs[i]
+                    po = psum.tile([P, JB, P], F32, name="po", bufs=2)
+                    for jj in range(JB):
+                        cols = slice(jj * P, (jj + 1) * P)
+                        nc.tensor.matmul(
+                            out=po[:, jj, :], lhsT=first[:, cols], rhs=ident32[:], is_transpose=True, start=True, stop=False)
+                        nc.tensor.matmul(
+                            out=po[:, jj, :], lhsT=second[:, cols], rhs=ident32[:], is_transpose=True, start=False, stop=True)
+                    if i in VECTOR_EVACS:
+                        nc.vector.tensor_copy(out=o_t[i][:, :, hs], in_=po[:])
+                    else:
+                        nc.scalar.copy(out=o_t[i][:, :, hs], in_=po[:])
             for i in range(5):
                 nc.sync.dma_start(out=out_v[i][:, js, :], in_=o_t[i][:])

@@ -22,7 +22,6 @@ NB = NJ // JB
 R = JB * P
 NH = D // P
 FLOPS = 2 * B * E * D * 2
-VECTOR_EVACS = ()
 
 
 def tile_rwkv_timemix_for_quant_pa_t_kernel(
@@ -65,17 +64,18 @@ def tile_rwkv_timemix_for_quant_pa_t_kernel(
         nc.tensor.transpose(vecs_t[:], vecs[:], ident[:])
         cst = const.tile([P, 12], F32, name="cst")
         nc.vector.tensor_copy(out=cst[:], in_=vecs_t[:, 0:12])
-        mix = cst[:, 0:8]
         omix = const.tile([P, 8], F32, name="omix")
-        nc.vector.tensor_scalar(out=omix[:], in0=mix, scalar1=-1.0, scalar2=1.0, op0=ALU.mult, op1=ALU.add)
+        nc.vector.tensor_scalar(out=omix[:], in0=cst[:, 0:8], scalar1=-1.0, scalar2=1.0, op0=ALU.mult, op1=ALU.add)
         ed = const.tile([P, NH], F32, name="ed")
         nc.scalar.activation(out=ed[:], in_=cst[:, 10:12], func=ACT.Exp)
         td = const.tile([P, NH], F32, name="td")
         nc.vector.tensor_scalar(out=td[:], in0=ed[:], scalar1=-1.0, scalar2=None, op0=ALU.mult)
         c1 = const.tile([P, NH], F32, name="c1")
         nc.vector.tensor_tensor(out=c1[:], in0=ed[:], in1=cst[:, 8:10], op=ALU.subtract)
-        nc1 = const.tile([P, NH], F32, name="nc1")
-        nc.vector.tensor_scalar(out=nc1[:], in0=c1[:], scalar1=-1.0, scalar2=None, op0=ALU.mult)
+        c1t = const.tile([P, NH, P], F32, name="c1t")
+        nc.vector.memset(c1t[:], 0.0)
+        for h in range(NH):
+            nc.vector.tensor_scalar(out=c1t[:, h, :], in0=c1t[:, h, :], scalar1=c1[:, h:h + 1], scalar2=None, op0=ALU.add)
 
         w_codes = []
         w_scales = []
@@ -92,7 +92,7 @@ def tile_rwkv_timemix_for_quant_pa_t_kernel(
             w_codes.append(wc)
             w_scales.append(ws)
 
-        for b in range(NB):
+        def front(b):
             js = slice(b * JB, (b + 1) * JB)
             x_sb = loads.tile([P, JB, E], BF16, name="x_sb")
             nc.sync.dma_start(out=x_sb[:], in_=x_v[:, js, :])
@@ -104,6 +104,14 @@ def tile_rwkv_timemix_for_quant_pa_t_kernel(
             nc.sync.dma_start(out=sa_sb[:], in_=sa_v[:, js, :])
             sb_sb = loads.tile([P, JB, D], BF16, name="sb_sb")
             nc.sync.dma_start(out=sb_sb[:], in_=sb_v[:, js, :])
+
+            spT = psum.tile([P, NH, R], BF16, name="spT", tag="sxT", bufs=2)
+            for h in range(NH):
+                for jj in range(JB):
+                    nc.tensor.transpose(spT[:, h, jj * P:(jj + 1) * P], sp_sb[:, jj, h * P:(h + 1) * P], ident[:])
+            q2 = work.tile([P, NH, R], F32, name="q2")
+            for h in range(NH):
+                nc.scalar.activation(out=q2[:, h, :], in_=spT[:, h, :], func=ACT.Identity, bias=td[:, h:h + 1])
 
             planes = [work.tile([P, PACK, R], BF16, name="plane%d" % m) for m in range(2)]
             for hf in range(2):
@@ -131,7 +139,7 @@ def tile_rwkv_timemix_for_quant_pa_t_kernel(
             scales = []
             for m in range(2):
                 grouped = work.tile([P, R, PACK], BF16, name="grouped%d" % m, align_bytes=64)
-                nc.vector.tensor_copy(
+                nc.scalar.copy(
                     out=grouped[:].rearrange("p (c i) t -> p c t i", i=4),
                     in_=planes[m][:].rearrange("p t (c i) -> p c t i", i=4))
                 codes.append(work.tile([P, R], U32, name="cd%d" % m, align_bytes=64))
@@ -139,68 +147,74 @@ def tile_rwkv_timemix_for_quant_pa_t_kernel(
                 nc.vector.quantize_mx(
                     out=codes[m][:].bitcast(FP8X4), scales=scales[m][:], in_=grouped[:].rearrange("p r t -> p (r t)"))
 
-            spT = psum.tile([P, NH, R], BF16, name="spT", tag="sxT", bufs=2)
-            for h in range(NH):
-                for jj in range(JB):
-                    nc.tensor.transpose(spT[:, h, jj * P:(jj + 1) * P], sp_sb[:, jj, h * P:(h + 1) * P], ident[:])
-            q2 = work.tile([P, NH, R], F32, name="q2")
-            for h in range(NH):
-                nc.scalar.activation(out=q2[:, h, :], in_=spT[:, h, :], func=ACT.Identity, bias=td[:, h:h + 1])
-
-            o_t = [outs.tile([P, JB, D], F32, name="o%d" % i) for i in range(5)]
+            d2 = work.tile([P, NH, R], F32, name="d2")
+            r2 = work.tile([P, NH, R], F32, name="r2")
             for h in range(NH):
                 hs = slice(h * P, (h + 1) * P)
-                sabT = psum.tile([P, 2, R], BF16, name="sabT")
-                for si, s_sb in enumerate((sa_sb, sb_sb)):
-                    for jj in range(JB):
-                        nc.tensor.transpose(sabT[:, si, jj * P:(jj + 1) * P], s_sb[:, jj, hs], ident[:])
-                kv = []
-                for m in range(2):
-                    acc = psum.tile([P, R], F32, name="acc%d" % m)
+                k_ps = psum.tile([P, R], F32, name="k_ps")
+                nc.tensor.matmul_mx(
+                    out=k_ps[:], lhsT=w_codes[0][:, hs].bitcast(FP8X4), lhsT_scale=w_scales[0][:, hs],
+                    rhs=codes[0][:].bitcast(FP8X4), rhs_scale=scales[0][:], start=True, stop=True)
+                nc.vector.tensor_tensor(out=d2[:, h, :], in0=q2[:, h, :], in1=k_ps[:], op=ALU.subtract)
+                nc.scalar.activation(out=r2[:, h, :], in_=d2[:, h, :], func=ACT.Relu, scale=-1.0)
+            return (js, sa_sb, sb_sb, q2, d2, r2, codes[1], scales[1])
+
+        def back(state):
+            js, sa_sb, sb_sb, q2, d2, r2, v_codes, v_scales = state
+            o_t = [outs.tile([P, JB, D], F32, name="o%d" % i) for i in range(5)]
+            for pr in range(JB // 2):
+                ps = slice(2 * pr, 2 * pr + 2)
+                dl2 = psum.tile([P, 2, D], F32, name="dl2")
+                dl1 = psum.tile([P, 2, D], F32, name="dl1")
+                po = psum.tile([P, 2, D], F32, name="po")
+                v_ps = psum.tile([P, 2, D], F32, name="v_ps")
+                for j2 in range(2):
+                    cols = slice((2 * pr + j2) * P, (2 * pr + j2 + 1) * P)
+                    for h in range(NH):
+                        nc.tensor.transpose(dl2[:, j2, h * P:(h + 1) * P], d2[:, h, cols], ident32[:])
+                for j2 in range(2):
+                    cols = slice((2 * pr + j2) * P, (2 * pr + j2 + 1) * P)
+                    for h in range(NH):
+                        hs = slice(h * P, (h + 1) * P)
+                        nc.tensor.matmul(
+                            out=dl1[:, j2, hs], lhsT=d2[:, h, cols], rhs=ident32[:], is_transpose=True, start=True, stop=False)
+                        nc.tensor.matmul(
+                            out=dl1[:, j2, hs], lhsT=c1t[:, h, :], rhs=ident32[:], is_transpose=True, start=False, stop=True)
+                for j2 in range(2):
+                    cols = slice((2 * pr + j2) * P, (2 * pr + j2 + 1) * P)
+                    for h in range(NH):
+                        hs = slice(h * P, (h + 1) * P)
+                        nc.tensor.matmul(
+                            out=po[:, j2, hs], lhsT=q2[:, h, cols], rhs=ident32[:], is_transpose=True, start=True, stop=False)
+                        nc.tensor.matmul(
+                            out=po[:, j2, hs], lhsT=r2[:, h, cols], rhs=ident32[:], is_transpose=True, start=False, stop=True)
+                for j2 in range(2):
+                    cols = slice((2 * pr + j2) * P, (2 * pr + j2 + 1) * P)
                     nc.tensor.matmul_mx(
-                        out=acc[:], lhsT=w_codes[m][:, hs].bitcast(FP8X4), lhsT_scale=w_scales[m][:, hs],
-                        rhs=codes[m][:].bitcast(FP8X4), rhs_scale=scales[m][:], start=True, stop=True)
-                    kv.append(acc)
-                k_ps, v_ps = kv
-                d2 = work.tile([P, R], F32, name="d2")
-                nc.vector.tensor_tensor(out=d2[:], in0=q2[:, h, :], in1=k_ps[:], op=ALU.subtract)
-                r2 = work.tile([P, R], F32, name="r2")
-                nc.scalar.activation(out=r2[:], in_=d2[:], func=ACT.Relu, scale=-1.0)
-                pairs = [None, None, None, None, (q2[:, h, :], r2[:])]
-                for half in range(2):
-                    ep = work.tile([P, R], F32, name="ep%d" % half)
-                    em = work.tile([P, R], F32, name="em%d" % half)
-                    if half == 0:
-                        nc.scalar.activation(out=ep[:], in_=d2[:], func=ACT.Exp, bias=c1[:, h:h + 1])
-                        nc.scalar.activation(out=em[:], in_=d2[:], func=ACT.Exp, bias=nc1[:, h:h + 1], scale=-1.0)
-                    else:
-                        nc.scalar.activation(out=ep[:], in_=d2[:], func=ACT.Exp)
-                        nc.scalar.activation(out=em[:], in_=d2[:], func=ACT.Exp, scale=-1.0)
-                    t1 = work.tile([P, R], F32, name="t1_%d" % half)
+                        out=v_ps[:, j2, :], lhsT=v_codes[:, cols].bitcast(FP8X4), lhsT_scale=v_scales[:, cols],
+                        rhs=w_codes[1][:].bitcast(FP8X4), rhs_scale=w_scales[1][:], start=True, stop=True)
+                nc.scalar.copy(out=o_t[4][:, ps, :], in_=po[:])
+                sa = sa_sb[:, ps, :]
+                sb = sb_sb[:, ps, :]
+                for half, dl in ((1, dl2), (0, dl1)):
+                    ep = work.tile([P, 2, D], F32, name="ep%d" % half)
+                    nc.scalar.activation(out=ep[:], in_=dl[:], func=ACT.Exp)
+                    em = work.tile([P, 2, D], F32, name="em%d" % half)
+                    nc.scalar.activation(out=em[:], in_=dl[:], func=ACT.Exp, scale=-1.0)
+                    t1 = work.tile([P, 2, D], F32, name="t1_%d" % half)
+                    nc.vector.scalar_tensor_tensor(out=t1[:], in0=ep[:], scalar=1.0, in1=sa, op0=ALU.min, op1=ALU.mult)
+                    t3 = work.tile([P, 2, D], F32, name="t3_%d" % half)
+                    nc.vector.scalar_tensor_tensor(out=t3[:], in0=ep[:], scalar=1.0, in1=sb, op0=ALU.min, op1=ALU.mult)
+                    t2 = work.tile([P, 2, D], F32, name="t2_%d" % half)
+                    nc.vector.scalar_tensor_tensor(out=t2[:], in0=em[:], scalar=1.0, in1=v_ps[:], op0=ALU.min, op1=ALU.mult)
                     nc.vector.scalar_tensor_tensor(
-                        out=t1[:], in0=ep[:], scalar=1.0, in1=sabT[:, 0, :], op0=ALU.min, op1=ALU.mult)
-                    t3 = work.tile([P, R], F32, name="t3_%d" % half)
-                    nc.vector.scalar_tensor_tensor(
-                        out=t3[:], in0=ep[:], scalar=1.0, in1=sabT[:, 1, :], op0=ALU.min, op1=ALU.mult)
-                    t2 = work.tile([P, R], F32, name="t2_%d" % half)
-                    nc.vector.scalar_tensor_tensor(
-                        out=t2[:], in0=em[:], scalar=1.0, in1=v_ps[:], op0=ALU.min, op1=ALU.mult)
-                    e2 = work.tile([P, R], F32, name="e2_%d" % half)
-                    nc.vector.tensor_scalar(out=e2[:], in0=em[:], scalar1=1.0, scalar2=None, op0=ALU.min)
-                    pairs[2 * half] = (t1[:], t2[:])
-                    pairs[2 * half + 1] = (t3[:], e2[:])
-                for i in (4, 0, 1, 2, 3):
-                    first, second = pairs[i]
-                    po = psum.tile([P, JB, P], F32, name="po", bufs=2)
-                    for jj in range(JB):
-                        cols = slice(jj * P, (jj + 1) * P)
-                        nc.tensor.matmul(
-                            out=po[:, jj, :], lhsT=first[:, cols], rhs=ident32[:], is_transpose=True, start=True, stop=False)
-                        nc.tensor.matmul(
-                            out=po[:, jj, :], lhsT=second[:, cols], rhs=ident32[:], is_transpose=True, start=False, stop=True)
-                    if i in VECTOR_EVACS:
-                        nc.vector.tensor_copy(out=o_t[i][:, :, hs], in_=po[:])
-                    else:
-                        nc.scalar.copy(out=o_t[i][:, :, hs], in_=po[:])
+                        out=o_t[2 * half + 1][:, ps, :], in0=em[:], scalar=1.0, in1=t3[:], op0=ALU.min, op1=ALU.add)
+                    nc.vector.tensor_tensor(out=o_t[2 * half][:, ps, :], in0=t1[:], in1=t2[:], op=ALU.add)
             for i in range(5):
                 nc.sync.dma_start(out=out_v[i][:, js, :], in_=o_t[i][:])
+
+        state = front(0)
+        for b in range(NB):
+            following = front(b + 1) if b + 1 < NB else None
+            back(state)
+            state = following

@@ -33,6 +33,7 @@ def tile_rwkv_timemix_for_quant_pa_t_kernel(
         const = ctx.enter_context(tc.tile_pool(name="const", bufs=1))
         loads = ctx.enter_context(tc.tile_pool(name="loads", bufs=3))
         work = ctx.enter_context(tc.tile_pool(name="work", bufs=2))
+        single = ctx.enter_context(tc.tile_pool(name="single", bufs=1))
         outs = ctx.enter_context(tc.tile_pool(name="outs", bufs=2))
         psum = ctx.enter_context(tc.psum_pool(name="psum", bufs=1))
 
@@ -48,22 +49,27 @@ def tile_rwkv_timemix_for_quant_pa_t_kernel(
         ident32 = const.tile([P, P], F32, name="ident32")
         make_identity(nc, ident32[:])
 
+        mixrows = const.tile([P, 2 * P], BF16, name="mixrows")
+        nc.vector.memset(mixrows[:], 0.0)
+        nc.sync.dma_start(out=mixrows[0:2, :], in_=time_mix_k.rearrange("o (u w) -> (o u) w", u=2))
+        nc.sync.dma_start(out=mixrows[2:4, :], in_=time_mix_v.rearrange("o (u w) -> (o u) w", u=2))
         vecs = const.tile([P, P], BF16, name="vecs")
         nc.vector.memset(vecs[:], 0.0)
-        nc.sync.dma_start(out=vecs[0:4, :], in_=time_mix_k.rearrange("o (t p) -> (o t) p", p=P))
-        nc.sync.dma_start(out=vecs[4:8, :], in_=time_mix_v.rearrange("o (t p) -> (o t) p", p=P))
-        nc.sync.dma_start(out=vecs[8:10, :], in_=time_first.rearrange("(h p) -> h p", p=P))
-        nc.sync.dma_start(out=vecs[10:12, :], in_=time_decay.rearrange("(h p) -> h p", p=P))
+        nc.sync.dma_start(out=vecs[0:2, :], in_=time_first.rearrange("(h p) -> h p", p=P))
+        nc.sync.dma_start(out=vecs[2:4, :], in_=time_decay.rearrange("(h p) -> h p", p=P))
         w_sb = []
         for wi, w in enumerate((W_key, W_value)):
             wt = const.tile([P, NH, E], BF16, name="w_sb%d" % wi)
             nc.sync.dma_start(out=wt[:], in_=w.rearrange("(h p) k -> p h k", p=P))
             w_sb.append(wt)
 
-        vecs_t = psum.tile([P, P], BF16, name="vecs_t", tag="xT")
+        mix_t = psum.tile([P, P], F32, name="mix_t", tag="xT", bufs=2)
+        nc.tensor.transpose(mix_t[:], mixrows[:].bitcast(F32), ident32[:])
+        vecs_t = psum.tile([P, P], BF16, name="vecs_t", tag="xT", bufs=2)
         nc.tensor.transpose(vecs_t[:], vecs[:], ident[:])
         cst = const.tile([P, 12], F32, name="cst")
-        nc.vector.tensor_copy(out=cst[:], in_=vecs_t[:, 0:12])
+        nc.vector.tensor_copy(out=cst[:, 0:8], in_=mix_t[:].bitcast(BF16)[:, 0:8])
+        nc.vector.tensor_copy(out=cst[:, 8:12], in_=vecs_t[:, 0:4])
         omix = const.tile([P, 8], F32, name="omix")
         nc.vector.tensor_scalar(out=omix[:], in0=cst[:, 0:8], scalar1=-1.0, scalar2=1.0, op0=ALU.mult, op1=ALU.add)
         ed = const.tile([P, NH], F32, name="ed")
@@ -80,12 +86,15 @@ def tile_rwkv_timemix_for_quant_pa_t_kernel(
         w_codes = []
         w_scales = []
         for wi in range(2):
-            w_t = psum.tile([P, PACK, D], BF16, name="w_t%d" % wi, tag="sxT", bufs=2)
+            w_t = psum.tile([P, 2, D], F32, name="w_t%d" % wi, tag="sxT", bufs=2)
             for h in range(NH):
-                for t in range(PACK):
-                    nc.tensor.transpose(w_t[:, t, h * P:(h + 1) * P], w_sb[wi][:, h, t * P:(t + 1) * P], ident[:])
+                for u in range(2):
+                    nc.tensor.transpose(
+                        w_t[:, u, h * P:(h + 1) * P], w_sb[wi][:, h, :].bitcast(F32)[:, u * P:(u + 1) * P], ident32[:])
             wg = const.tile([P, D, PACK], BF16, name="wg%d" % wi, align_bytes=64)
-            nc.vector.tensor_copy(out=wg[:], in_=w_t[:].rearrange("p t d -> p d t"))
+            nc.vector.tensor_copy(
+                out=wg[:].rearrange("p d t -> p (d t)").bitcast(F32).rearrange("p (d u) -> p d u", u=2),
+                in_=w_t[:].rearrange("p u d -> p d u"))
             wc = const.tile([P, D], U32, name="wc%d" % wi, align_bytes=64)
             ws = const.tile([P, D], U8, name="ws%d" % wi, align_bytes=64)
             nc.vector.quantize_mx(out=wc[:].bitcast(FP8X4), scales=ws[:], in_=wg[:].rearrange("p d t -> p (d t)"))
@@ -100,10 +109,9 @@ def tile_rwkv_timemix_for_quant_pa_t_kernel(
             nc.sync.dma_start(out=sx_sb[:], in_=sx_v[:, js, :])
             sp_sb = loads.tile([P, JB, D], BF16, name="sp_sb")
             nc.sync.dma_start(out=sp_sb[:], in_=sp_v[:, js, :])
-            sa_sb = loads.tile([P, JB, D], BF16, name="sa_sb")
-            nc.sync.dma_start(out=sa_sb[:], in_=sa_v[:, js, :])
-            sb_sb = loads.tile([P, JB, D], BF16, name="sb_sb")
-            nc.sync.dma_start(out=sb_sb[:], in_=sb_v[:, js, :])
+            sab = loads.tile([P, 2, JB, D], BF16, name="sab")
+            nc.sync.dma_start(out=sab[:, 0, :, :], in_=sa_v[:, js, :])
+            nc.sync.dma_start(out=sab[:, 1, :, :], in_=sb_v[:, js, :])
 
             spT = psum.tile([P, NH, R], BF16, name="spT", tag="sxT", bufs=2)
             for h in range(NH):
@@ -113,32 +121,32 @@ def tile_rwkv_timemix_for_quant_pa_t_kernel(
             for h in range(NH):
                 nc.scalar.activation(out=q2[:, h, :], in_=spT[:, h, :], func=ACT.Identity, bias=td[:, h:h + 1])
 
-            planes = [work.tile([P, PACK, R], BF16, name="plane%d" % m) for m in range(2)]
-            for hf in range(2):
-                sxT = psum.tile([P, 2, R], BF16, name="sxT", tag="sxT", bufs=2)
-                xT = psum.tile([P, 2, R], BF16, name="xT", tag="xT")
-                for tt in range(2):
-                    t = 2 * hf + tt
-                    for jj in range(JB):
-                        nc.tensor.transpose(sxT[:, tt, jj * P:(jj + 1) * P], sx_sb[:, jj, t * P:(t + 1) * P], ident[:])
-                for tt in range(2):
-                    t = 2 * hf + tt
-                    for jj in range(JB):
-                        nc.tensor.transpose(xT[:, tt, jj * P:(jj + 1) * P], x_sb[:, jj, t * P:(t + 1) * P], ident[:])
+            planes = [single.tile([P, PACK, R], BF16, name="plane%d" % m) for m in range(2)]
+            for u in range(2):
+                sxT = psum.tile([P, R], F32, name="sxT", tag="sxT", bufs=2)
+                xT = psum.tile([P, R], F32, name="xT", tag="xT", bufs=2)
+                for jj in range(JB):
+                    nc.tensor.transpose(
+                        sxT[:, jj * P:(jj + 1) * P], sx_sb[:, jj, :].bitcast(F32)[:, u * P:(u + 1) * P], ident32[:])
+                for jj in range(JB):
+                    nc.tensor.transpose(
+                        xT[:, jj * P:(jj + 1) * P], x_sb[:, jj, :].bitcast(F32)[:, u * P:(u + 1) * P], ident32[:])
+                sx_pair = sxT[:].bitcast(BF16).rearrange("p (r e) -> p r e", e=2)
+                x_pair = xT[:].bitcast(BF16).rearrange("p (r e) -> p r e", e=2)
                 for m in range(2):
-                    u = work.tile([P, 2, R], F32, name="u%d" % m)
-                    for tt in range(2):
-                        t = 2 * hf + tt
+                    prod = work.tile([P, 2, R], F32, name="prod%d" % m)
+                    for e in range(2):
+                        t = 2 * u + e
                         c = 4 * m + t
-                        nc.scalar.activation(out=u[:, tt, :], in_=sxT[:, tt, :], func=ACT.Copy, scale=omix[:, c:c + 1])
+                        nc.scalar.activation(out=prod[:, e, :], in_=sx_pair[:, :, e], func=ACT.Copy, scale=omix[:, c:c + 1])
                         nc.vector.scalar_tensor_tensor(
-                            out=planes[m][:, t, :], in0=xT[:, tt, :], scalar=cst[:, c:c + 1], in1=u[:, tt, :],
+                            out=planes[m][:, t, :], in0=x_pair[:, :, e], scalar=cst[:, c:c + 1], in1=prod[:, e, :],
                             op0=ALU.mult, op1=ALU.add)
 
             codes = []
             scales = []
             for m in range(2):
-                grouped = work.tile([P, R, PACK], BF16, name="grouped%d" % m, align_bytes=64)
+                grouped = single.tile([P, R, PACK], BF16, name="grouped%d" % m, align_bytes=64)
                 nc.scalar.copy(
                     out=grouped[:].rearrange("p (c i) t -> p c t i", i=4),
                     in_=planes[m][:].rearrange("p t (c i) -> p c t i", i=4))
@@ -151,22 +159,25 @@ def tile_rwkv_timemix_for_quant_pa_t_kernel(
             r2 = work.tile([P, NH, R], F32, name="r2")
             for h in range(NH):
                 hs = slice(h * P, (h + 1) * P)
-                k_ps = psum.tile([P, R], F32, name="k_ps")
+                k_ps = psum.tile([P, R], F32, name="k_ps", tag="kp")
                 nc.tensor.matmul_mx(
                     out=k_ps[:], lhsT=w_codes[0][:, hs].bitcast(FP8X4), lhsT_scale=w_scales[0][:, hs],
                     rhs=codes[0][:].bitcast(FP8X4), rhs_scale=scales[0][:], start=True, stop=True)
                 nc.vector.tensor_tensor(out=d2[:, h, :], in0=q2[:, h, :], in1=k_ps[:], op=ALU.subtract)
-                nc.scalar.activation(out=r2[:, h, :], in_=d2[:, h, :], func=ACT.Relu, scale=-1.0)
-            return (js, sa_sb, sb_sb, q2, d2, r2, codes[1], scales[1])
+            nc.scalar.activation(out=r2[:], in_=d2[:], func=ACT.Relu, scale=-1.0)
+            return (js, sab, q2, d2, r2, codes[1], scales[1])
 
         def back(state):
-            js, sa_sb, sb_sb, q2, d2, r2, v_codes, v_scales = state
+            js, sab, q2, d2, r2, v_codes, v_scales = state
             o_t = [outs.tile([P, JB, D], F32, name="o%d" % i) for i in range(5)]
+            ep = [work.tile([P, JB, D], F32, name="ep%d" % half) for half in range(2)]
+            em = [work.tile([P, JB, D], F32, name="em%d" % half) for half in range(2)]
+            t2 = [single.tile([P, JB, D], F32, name="t2_%d" % half) for half in range(2)]
             for pr in range(JB // 2):
                 ps = slice(2 * pr, 2 * pr + 2)
                 dl2 = psum.tile([P, 2, D], F32, name="dl2")
                 dl1 = psum.tile([P, 2, D], F32, name="dl1")
-                po = psum.tile([P, 2, D], F32, name="po")
+                po = psum.tile([P, 2, D], F32, name="po", tag="kp")
                 v_ps = psum.tile([P, 2, D], F32, name="v_ps")
                 for j2 in range(2):
                     cols = slice((2 * pr + j2) * P, (2 * pr + j2 + 1) * P)
@@ -194,22 +205,22 @@ def tile_rwkv_timemix_for_quant_pa_t_kernel(
                         out=v_ps[:, j2, :], lhsT=v_codes[:, cols].bitcast(FP8X4), lhsT_scale=v_scales[:, cols],
                         rhs=w_codes[1][:].bitcast(FP8X4), rhs_scale=w_scales[1][:], start=True, stop=True)
                 nc.scalar.copy(out=o_t[4][:, ps, :], in_=po[:])
-                sa = sa_sb[:, ps, :]
-                sb = sb_sb[:, ps, :]
                 for half, dl in ((1, dl2), (0, dl1)):
-                    ep = work.tile([P, 2, D], F32, name="ep%d" % half)
-                    nc.scalar.activation(out=ep[:], in_=dl[:], func=ACT.Exp)
-                    em = work.tile([P, 2, D], F32, name="em%d" % half)
-                    nc.scalar.activation(out=em[:], in_=dl[:], func=ACT.Exp, scale=-1.0)
-                    t1 = work.tile([P, 2, D], F32, name="t1_%d" % half)
-                    nc.vector.scalar_tensor_tensor(out=t1[:], in0=ep[:], scalar=1.0, in1=sa, op0=ALU.min, op1=ALU.mult)
-                    t3 = work.tile([P, 2, D], F32, name="t3_%d" % half)
-                    nc.vector.scalar_tensor_tensor(out=t3[:], in0=ep[:], scalar=1.0, in1=sb, op0=ALU.min, op1=ALU.mult)
-                    t2 = work.tile([P, 2, D], F32, name="t2_%d" % half)
-                    nc.vector.scalar_tensor_tensor(out=t2[:], in0=em[:], scalar=1.0, in1=v_ps[:], op0=ALU.min, op1=ALU.mult)
+                    nc.scalar.activation(out=ep[half][:, ps, :], in_=dl[:], func=ACT.Exp)
+                    nc.scalar.activation(out=em[half][:, ps, :], in_=dl[:], func=ACT.Exp, scale=-1.0)
                     nc.vector.scalar_tensor_tensor(
-                        out=o_t[2 * half + 1][:, ps, :], in0=em[:], scalar=1.0, in1=t3[:], op0=ALU.min, op1=ALU.add)
-                    nc.vector.tensor_tensor(out=o_t[2 * half][:, ps, :], in0=t1[:], in1=t2[:], op=ALU.add)
+                        out=t2[half][:, ps, :], in0=em[half][:, ps, :], scalar=1.0, in1=v_ps[:], op0=ALU.min, op1=ALU.mult)
+            for half in (1, 0):
+                t13 = single.tile([P, 2, JB * D], F32, name="t13_%d" % half)
+                nc.vector.scalar_tensor_tensor(
+                    out=t13[:], in0=ep[half][:].rearrange("p j d -> p (j d)").unsqueeze(1).to_broadcast([P, 2, JB * D]),
+                    scalar=1.0, in1=sab[:].rearrange("p s j d -> p s (j d)"), op0=ALU.min, op1=ALU.mult)
+                nc.vector.scalar_tensor_tensor(
+                    out=o_t[2 * half + 1][:].rearrange("p j d -> p (j d)"), in0=em[half][:].rearrange("p j d -> p (j d)"),
+                    scalar=1.0, in1=t13[:, 1, :], op0=ALU.min, op1=ALU.add)
+                nc.vector.tensor_tensor(
+                    out=o_t[2 * half][:].rearrange("p j d -> p (j d)"), in0=t13[:, 0, :],
+                    in1=t2[half][:].rearrange("p j d -> p (j d)"), op=ALU.add)
             for i in range(5):
                 nc.sync.dma_start(out=out_v[i][:, js, :], in_=o_t[i][:])
 

@@ -101,131 +101,237 @@ def tile_rwkv_timemix_for_quant_pa_t_kernel(
             w_codes.append(wc)
             w_scales.append(ws)
 
-        def front(b):
-            js = slice(b * JB, (b + 1) * JB)
-            x_sb = loads.tile([P, JB, E], BF16, name="x_sb")
-            nc.sync.dma_start(out=x_sb[:], in_=x_v[:, js, :])
-            sx_sb = loads.tile([P, JB, E], BF16, name="sx_sb")
-            nc.sync.dma_start(out=sx_sb[:], in_=sx_v[:, js, :])
-            sp_sb = loads.tile([P, JB, D], BF16, name="sp_sb")
-            nc.sync.dma_start(out=sp_sb[:], in_=sp_v[:, js, :])
-            sab = loads.tile([P, 2, JB, D], BF16, name="sab")
-            nc.sync.dma_start(out=sab[:, 0, :, :], in_=sa_v[:, js, :])
-            nc.sync.dma_start(out=sab[:, 1, :, :], in_=sb_v[:, js, :])
+        st = {}
 
-            spT = psum.tile([P, NH, R], BF16, name="spT", tag="sxT", bufs=2)
-            for h in range(NH):
-                for jj in range(JB):
-                    nc.tensor.transpose(spT[:, h, jj * P:(jj + 1) * P], sp_sb[:, jj, h * P:(h + 1) * P], ident[:])
-            q2 = work.tile([P, NH, R], F32, name="q2")
-            for h in range(NH):
-                nc.scalar.activation(out=q2[:, h, :], in_=spT[:, h, :], func=ACT.Identity, bias=td[:, h:h + 1])
+        def live(k):
+            return 0 <= k < NB
 
-            planes = [single.tile([P, PACK, R], BF16, name="plane%d" % m) for m in range(2)]
-            for u in range(2):
-                sxT = psum.tile([P, R], F32, name="sxT", tag="sxT", bufs=2)
-                xT = psum.tile([P, R], F32, name="xT", tag="xT", bufs=2)
-                for jj in range(JB):
-                    nc.tensor.transpose(
-                        sxT[:, jj * P:(jj + 1) * P], sx_sb[:, jj, :].bitcast(F32)[:, u * P:(u + 1) * P], ident32[:])
+        def rows(k):
+            return slice(k * JB, (k + 1) * JB)
+
+        def load_front(k):
+            st["x", k] = loads.tile([P, JB, E], BF16, name="x_sb")
+            nc.sync.dma_start(out=st["x", k][:], in_=x_v[:, rows(k), :])
+            st["sx", k] = loads.tile([P, JB, E], BF16, name="sx_sb")
+            nc.sync.dma_start(out=st["sx", k][:], in_=sx_v[:, rows(k), :])
+            st["sp", k] = loads.tile([P, JB, D], BF16, name="sp_sb", bufs=2)
+            nc.sync.dma_start(out=st["sp", k][:], in_=sp_v[:, rows(k), :])
+
+        def load_states(k):
+            st["sab", k] = loads.tile([P, 2, JB, D], BF16, name="sab", bufs=2)
+            nc.sync.dma_start(out=st["sab", k][:, 0, :, :], in_=sa_v[:, rows(k), :])
+            nc.sync.dma_start(out=st["sab", k][:, 1, :, :], in_=sb_v[:, rows(k), :])
+
+        def transpose_x(k, u):
+            st["sxT", k, u] = psum.tile([P, R], F32, name="sxT", tag="sxT", bufs=2)
+            st["xT", k, u] = psum.tile([P, R], F32, name="xT", tag="xT", bufs=2)
+            for key, src in (("sxT", "sx"), ("xT", "x")):
                 for jj in range(JB):
                     nc.tensor.transpose(
-                        xT[:, jj * P:(jj + 1) * P], x_sb[:, jj, :].bitcast(F32)[:, u * P:(u + 1) * P], ident32[:])
-                sx_pair = sxT[:].bitcast(BF16).rearrange("p (r e) -> p r e", e=2)
-                x_pair = xT[:].bitcast(BF16).rearrange("p (r e) -> p r e", e=2)
-                for m in range(2):
-                    prod = work.tile([P, 2, R], F32, name="prod%d" % m)
-                    for e in range(2):
-                        t = 2 * u + e
-                        c = 4 * m + t
-                        nc.scalar.activation(out=prod[:, e, :], in_=sx_pair[:, :, e], func=ACT.Copy, scale=omix[:, c:c + 1])
-                        nc.vector.scalar_tensor_tensor(
-                            out=planes[m][:, t, :], in0=x_pair[:, :, e], scalar=cst[:, c:c + 1], in1=prod[:, e, :],
-                            op0=ALU.mult, op1=ALU.add)
+                        st[key, k, u][:, jj * P:(jj + 1) * P], st[src, k][:, jj, :].bitcast(F32)[:, u * P:(u + 1) * P],
+                        ident32[:])
 
-            codes = []
-            scales = []
+        def products(k, u):
+            pair = st["sxT", k, u][:].bitcast(BF16).rearrange("p (r e) -> p r e", e=2)
             for m in range(2):
-                grouped = single.tile([P, R, PACK], BF16, name="grouped%d" % m, align_bytes=64)
-                nc.scalar.copy(
-                    out=grouped[:].rearrange("p (c i) t -> p c t i", i=4),
-                    in_=planes[m][:].rearrange("p t (c i) -> p c t i", i=4))
-                codes.append(work.tile([P, R], U32, name="cd%d" % m, align_bytes=64))
-                scales.append(work.tile([P, R], U8, name="sc%d" % m, align_bytes=64))
-                nc.vector.quantize_mx(
-                    out=codes[m][:].bitcast(FP8X4), scales=scales[m][:], in_=grouped[:].rearrange("p r t -> p (r t)"))
+                st["prod", k, u, m] = work.tile([P, 2, R], F32, name="prod%d" % m)
+                for e in range(2):
+                    c = 4 * m + 2 * u + e
+                    nc.scalar.activation(
+                        out=st["prod", k, u, m][:, e, :], in_=pair[:, :, e], func=ACT.Copy, scale=omix[:, c:c + 1])
 
-            d2 = work.tile([P, NH, R], F32, name="d2")
-            r2 = work.tile([P, NH, R], F32, name="r2")
-            for h in range(NH):
-                hs = slice(h * P, (h + 1) * P)
-                k_ps = psum.tile([P, R], F32, name="k_ps", tag="kp")
-                nc.tensor.matmul_mx(
-                    out=k_ps[:], lhsT=w_codes[0][:, hs].bitcast(FP8X4), lhsT_scale=w_scales[0][:, hs],
-                    rhs=codes[0][:].bitcast(FP8X4), rhs_scale=scales[0][:], start=True, stop=True)
-                nc.vector.tensor_tensor(out=d2[:, h, :], in0=q2[:, h, :], in1=k_ps[:], op=ALU.subtract)
-            nc.scalar.activation(out=r2[:], in_=d2[:], func=ACT.Relu, scale=-1.0)
-            return (js, sab, q2, d2, r2, codes[1], scales[1])
-
-        def back(state):
-            js, sab, q2, d2, r2, v_codes, v_scales = state
-            o_t = [outs.tile([P, JB, D], F32, name="o%d" % i) for i in range(5)]
-            ep = [work.tile([P, JB, D], F32, name="ep%d" % half) for half in range(2)]
-            em = [work.tile([P, JB, D], F32, name="em%d" % half) for half in range(2)]
-            t2 = [single.tile([P, JB, D], F32, name="t2_%d" % half) for half in range(2)]
-            for pr in range(JB // 2):
-                ps = slice(2 * pr, 2 * pr + 2)
-                dl2 = psum.tile([P, 2, D], F32, name="dl2")
-                dl1 = psum.tile([P, 2, D], F32, name="dl1")
-                po = psum.tile([P, 2, D], F32, name="po", tag="kp")
-                v_ps = psum.tile([P, 2, D], F32, name="v_ps")
-                for j2 in range(2):
-                    cols = slice((2 * pr + j2) * P, (2 * pr + j2 + 1) * P)
-                    for h in range(NH):
-                        nc.tensor.transpose(dl2[:, j2, h * P:(h + 1) * P], d2[:, h, cols], ident32[:])
-                for j2 in range(2):
-                    cols = slice((2 * pr + j2) * P, (2 * pr + j2 + 1) * P)
-                    for h in range(NH):
-                        hs = slice(h * P, (h + 1) * P)
-                        nc.tensor.matmul(
-                            out=dl1[:, j2, hs], lhsT=d2[:, h, cols], rhs=ident32[:], is_transpose=True, start=True, stop=False)
-                        nc.tensor.matmul(
-                            out=dl1[:, j2, hs], lhsT=c1t[:, h, :], rhs=ident32[:], is_transpose=True, start=False, stop=True)
-                for j2 in range(2):
-                    cols = slice((2 * pr + j2) * P, (2 * pr + j2 + 1) * P)
-                    for h in range(NH):
-                        hs = slice(h * P, (h + 1) * P)
-                        nc.tensor.matmul(
-                            out=po[:, j2, hs], lhsT=q2[:, h, cols], rhs=ident32[:], is_transpose=True, start=True, stop=False)
-                        nc.tensor.matmul(
-                            out=po[:, j2, hs], lhsT=r2[:, h, cols], rhs=ident32[:], is_transpose=True, start=False, stop=True)
-                for j2 in range(2):
-                    cols = slice((2 * pr + j2) * P, (2 * pr + j2 + 1) * P)
-                    nc.tensor.matmul_mx(
-                        out=v_ps[:, j2, :], lhsT=v_codes[:, cols].bitcast(FP8X4), lhsT_scale=v_scales[:, cols],
-                        rhs=w_codes[1][:].bitcast(FP8X4), rhs_scale=w_scales[1][:], start=True, stop=True)
-                nc.scalar.copy(out=o_t[4][:, ps, :], in_=po[:])
-                for half, dl in ((1, dl2), (0, dl1)):
-                    nc.scalar.activation(out=ep[half][:, ps, :], in_=dl[:], func=ACT.Exp)
-                    nc.scalar.activation(out=em[half][:, ps, :], in_=dl[:], func=ACT.Exp, scale=-1.0)
+        def mix(k, u):
+            if u == 0:
+                for m in range(2):
+                    st["plane", k, m] = single.tile([P, PACK, R], BF16, name="plane%d" % m)
+            pair = st["xT", k, u][:].bitcast(BF16).rearrange("p (r e) -> p r e", e=2)
+            for m in range(2):
+                for e in range(2):
+                    t = 2 * u + e
+                    c = 4 * m + t
                     nc.vector.scalar_tensor_tensor(
-                        out=t2[half][:, ps, :], in0=em[half][:, ps, :], scalar=1.0, in1=v_ps[:], op0=ALU.min, op1=ALU.mult)
-            for half in (1, 0):
-                t13 = single.tile([P, 2, JB * D], F32, name="t13_%d" % half)
-                nc.vector.scalar_tensor_tensor(
-                    out=t13[:], in0=ep[half][:].rearrange("p j d -> p (j d)").unsqueeze(1).to_broadcast([P, 2, JB * D]),
-                    scalar=1.0, in1=sab[:].rearrange("p s j d -> p s (j d)"), op0=ALU.min, op1=ALU.mult)
-                nc.vector.scalar_tensor_tensor(
-                    out=o_t[2 * half + 1][:].rearrange("p j d -> p (j d)"), in0=em[half][:].rearrange("p j d -> p (j d)"),
-                    scalar=1.0, in1=t13[:, 1, :], op0=ALU.min, op1=ALU.add)
-                nc.vector.tensor_tensor(
-                    out=o_t[2 * half][:].rearrange("p j d -> p (j d)"), in0=t13[:, 0, :],
-                    in1=t2[half][:].rearrange("p j d -> p (j d)"), op=ALU.add)
-            for i in range(5):
-                nc.sync.dma_start(out=out_v[i][:, js, :], in_=o_t[i][:])
+                        out=st["plane", k, m][:, t, :], in0=pair[:, :, e], scalar=cst[:, c:c + 1],
+                        in1=st["prod", k, u, m][:, e, :], op0=ALU.mult, op1=ALU.add)
 
-        state = front(0)
-        for b in range(NB):
-            following = front(b + 1) if b + 1 < NB else None
-            back(state)
-            state = following
+        def regroup(k):
+            for m in range(2):
+                st["grouped", k, m] = single.tile([P, R, PACK], BF16, name="grouped%d" % m, align_bytes=64)
+                nc.scalar.copy(
+                    out=st["grouped", k, m][:].rearrange("p (c i) t -> p c t i", i=4),
+                    in_=st["plane", k, m][:].rearrange("p t (c i) -> p c t i", i=4))
+
+        def quantise(k, m):
+            st["cd", k, m] = work.tile([P, R], U32, name="cd%d" % m, align_bytes=64)
+            st["sc", k, m] = work.tile([P, R], U8, name="sc%d" % m, align_bytes=64)
+            nc.vector.quantize_mx(
+                out=st["cd", k, m][:].bitcast(FP8X4), scales=st["sc", k, m][:],
+                in_=st["grouped", k, m][:].rearrange("p r t -> p (r t)"))
+
+        def transpose_sp(k):
+            st["spT", k] = psum.tile([P, NH, R], BF16, name="spT", tag="sxT", bufs=2)
+            for h in range(NH):
+                for jj in range(JB):
+                    nc.tensor.transpose(
+                        st["spT", k][:, h, jj * P:(jj + 1) * P], st["sp", k][:, jj, h * P:(h + 1) * P], ident[:])
+
+        def shift_sp(k):
+            st["q2", k] = work.tile([P, NH, R], F32, name="q2")
+            for h in range(NH):
+                nc.scalar.activation(
+                    out=st["q2", k][:, h, :], in_=st["spT", k][:, h, :], func=ACT.Identity, bias=td[:, h:h + 1])
+
+        def key_pass(k, h):
+            hs = slice(h * P, (h + 1) * P)
+            st["k_ps", k, h] = psum.tile([P, R], F32, name="k_ps", tag="kp")
+            nc.tensor.matmul_mx(
+                out=st["k_ps", k, h][:], lhsT=w_codes[0][:, hs].bitcast(FP8X4), lhsT_scale=w_scales[0][:, hs],
+                rhs=st["cd", k, 0][:].bitcast(FP8X4), rhs_scale=st["sc", k, 0][:], start=True, stop=True)
+
+        def difference(k, h):
+            if h == 0:
+                st["d2", k] = work.tile([P, NH, R], F32, name="d2")
+            nc.vector.tensor_tensor(
+                out=st["d2", k][:, h, :], in0=st["q2", k][:, h, :], in1=st["k_ps", k, h][:], op=ALU.subtract)
+
+        def relu_part(k):
+            st["r2", k] = single.tile([P, NH, R], F32, name="r2")
+            nc.scalar.activation(out=st["r2", k][:], in_=st["d2", k][:], func=ACT.Relu, scale=-1.0)
+
+        def cols_of(pr, j2):
+            return slice((2 * pr + j2) * P, (2 * pr + j2 + 1) * P)
+
+        def arguments_back(k, pr):
+            st["dl2", k, pr] = psum.tile([P, 2, D], F32, name="dl2")
+            st["dl1", k, pr] = psum.tile([P, 2, D], F32, name="dl1")
+            for j2 in range(2):
+                for h in range(NH):
+                    nc.tensor.transpose(
+                        st["dl2", k, pr][:, j2, h * P:(h + 1) * P], st["d2", k][:, h, cols_of(pr, j2)], ident32[:])
+            for j2 in range(2):
+                for h in range(NH):
+                    hs = slice(h * P, (h + 1) * P)
+                    nc.tensor.matmul(
+                        out=st["dl1", k, pr][:, j2, hs], lhsT=st["d2", k][:, h, cols_of(pr, j2)], rhs=ident32[:],
+                        is_transpose=True, start=True, stop=False)
+                    nc.tensor.matmul(
+                        out=st["dl1", k, pr][:, j2, hs], lhsT=c1t[:, h, :], rhs=ident32[:],
+                        is_transpose=True, start=False, stop=True)
+
+        def new_p_back(k, pr):
+            st["po", k, pr] = psum.tile([P, 2, D], F32, name="po", tag="kp")
+            for j2 in range(2):
+                for h in range(NH):
+                    hs = slice(h * P, (h + 1) * P)
+                    nc.tensor.matmul(
+                        out=st["po", k, pr][:, j2, hs], lhsT=st["q2", k][:, h, cols_of(pr, j2)], rhs=ident32[:],
+                        is_transpose=True, start=True, stop=False)
+                    nc.tensor.matmul(
+                        out=st["po", k, pr][:, j2, hs], lhsT=st["r2", k][:, h, cols_of(pr, j2)], rhs=ident32[:],
+                        is_transpose=True, start=False, stop=True)
+
+        def value_pass(k, pr):
+            st["v_ps", k, pr] = psum.tile([P, 2, D], F32, name="v_ps")
+            for j2 in range(2):
+                cols = cols_of(pr, j2)
+                nc.tensor.matmul_mx(
+                    out=st["v_ps", k, pr][:, j2, :], lhsT=st["cd", k, 1][:, cols].bitcast(FP8X4),
+                    lhsT_scale=st["sc", k, 1][:, cols], rhs=w_codes[1][:].bitcast(FP8X4), rhs_scale=w_scales[1][:],
+                    start=True, stop=True)
+
+        def exponentials(k, pr):
+            ps = slice(2 * pr, 2 * pr + 2)
+            if pr == 0:
+                for half in range(2):
+                    st["ep", k, half] = work.tile([P, JB, D], F32, name="ep%d" % half)
+                    st["em", k, half] = work.tile([P, JB, D], F32, name="em%d" % half)
+                for i in range(5):
+                    st["o", k, i] = outs.tile([P, JB, D], F32, name="o%d" % i)
+            for half, key in ((1, "dl2"), (0, "dl1")):
+                nc.scalar.activation(out=st["em", k, half][:, ps, :], in_=st[key, k, pr][:], func=ACT.Exp, scale=-1.0)
+                nc.scalar.activation(out=st["ep", k, half][:, ps, :], in_=st[key, k, pr][:], func=ACT.Exp)
+            nc.scalar.copy(out=st["o", k, 4][:, ps, :], in_=st["po", k, pr][:])
+
+        def value_products(k, pr):
+            ps = slice(2 * pr, 2 * pr + 2)
+            for half in (1, 0):
+                if pr == 0:
+                    st["t2", k, half] = single.tile([P, JB, D], F32, name="t2_%d" % half)
+                nc.vector.scalar_tensor_tensor(
+                    out=st["t2", k, half][:, ps, :], in0=st["em", k, half][:, ps, :], scalar=1.0,
+                    in1=st["v_ps", k, pr][:], op0=ALU.min, op1=ALU.mult)
+
+        def state_products(k, half):
+            st["t13", k, half] = single.tile([P, 2, JB * D], F32, name="t13_%d" % half)
+            nc.vector.scalar_tensor_tensor(
+                out=st["t13", k, half][:],
+                in0=st["ep", k, half][:].rearrange("p j d -> p (j d)").unsqueeze(1).to_broadcast([P, 2, JB * D]),
+                scalar=1.0, in1=st["sab", k][:].rearrange("p s j d -> p s (j d)"), op0=ALU.min, op1=ALU.mult)
+
+        def sum_b(k, half):
+            nc.vector.scalar_tensor_tensor(
+                out=st["o", k, 2 * half + 1][:].rearrange("p j d -> p (j d)"),
+                in0=st["em", k, half][:].rearrange("p j d -> p (j d)"), scalar=1.0, in1=st["t13", k, half][:, 1, :],
+                op0=ALU.min, op1=ALU.add)
+
+        def sum_a(k, half):
+            nc.vector.tensor_tensor(
+                out=st["o", k, 2 * half][:].rearrange("p j d -> p (j d)"), in0=st["t13", k, half][:, 0, :],
+                in1=st["t2", k, half][:].rearrange("p j d -> p (j d)"), op=ALU.add)
+
+        def store(k):
+            for i in (4, 3, 2, 1, 0):
+                nc.sync.dma_start(out=out_v[i][:, rows(k), :], in_=st["o", k, i][:])
+
+        with tc.manual_schedule():
+            for i in range(-3, NB + 1):
+                prev, cur, nxt, nx2 = i - 1, i, i + 1, i + 2
+                if live(i + 3):
+                    load_front(i + 3)
+                if live(nxt):
+                    load_states(nxt)
+                    transpose_x(nxt, 1)
+                    products(nxt, 0)
+                if live(cur):
+                    relu_part(cur)
+                    new_p_back(cur, 0)
+                if live(nxt):
+                    mix(nxt, 0)
+                if live(nx2):
+                    transpose_sp(nx2)
+                if live(prev):
+                    sum_a(prev, 1)
+                    sum_b(prev, 0)
+                    sum_a(prev, 0)
+                    store(prev)
+                if live(cur):
+                    exponentials(cur, 0)
+                    value_products(cur, 0)
+                    arguments_back(cur, 1)
+                    value_pass(cur, 1)
+                    new_p_back(cur, 1)
+                if live(nxt):
+                    products(nxt, 1)
+                    mix(nxt, 1)
+                if live(nx2):
+                    transpose_x(nx2, 0)
+                if live(cur):
+                    exponentials(cur, 1)
+                    value_products(cur, 1)
+                    state_products(cur, 1)
+                    state_products(cur, 0)
+                if live(nxt):
+                    regroup(nxt)
+                    quantise(nxt, 0)
+                    key_pass(nxt, 0)
+                if live(cur):
+                    sum_b(cur, 1)
+                if live(nxt):
+                    difference(nxt, 0)
+                    quantise(nxt, 1)
+                    key_pass(nxt, 1)
+                    value_pass(nxt, 0)
+                    difference(nxt, 1)
+                if live(nx2):
+                    shift_sp(nx2)
+                if live(nxt):
+                    arguments_back(nxt, 0)

@@ -21,6 +21,7 @@ JB = 4
 NB = NJ // JB
 R = JB * P
 NH = D // P
+EXP_TOP = 80.0
 FLOPS = 2 * B * E * D * 2
 
 
@@ -44,6 +45,29 @@ def tile_rwkv_timemix_for_quant_pa_t_kernel(
         sp_v = state_p.rearrange("(p j) d -> p j d", j=NJ)
         out_v = [o.rearrange("(p j) d -> p j d", j=NJ) for o in (out_0, out_1, out_2, out_3, out_4)]
 
+        st = {}
+
+        def live(k):
+            return 0 <= k < NB
+
+        def rows(k):
+            return slice(k * JB, (k + 1) * JB)
+
+        def load_mixing(k):
+            st["sx", k] = loads.tile([P, JB, E], BF16, name="sx_sb")
+            nc.sync.dma_start(out=st["sx", k][:], in_=sx_v[:, rows(k), :])
+            st["x", k] = loads.tile([P, JB, E], BF16, name="x_sb")
+            nc.sync.dma_start(out=st["x", k][:], in_=x_v[:, rows(k), :])
+
+        def load_sp(k):
+            st["sp", k] = loads.tile([P, JB, D], BF16, name="sp_sb", bufs=2)
+            nc.sync.dma_start(out=st["sp", k][:], in_=sp_v[:, rows(k), :])
+
+        def load_states(k):
+            for s, view in enumerate((sa_v, sb_v)):
+                st["ab", k, s] = loads.tile([P, JB, D], BF16, name="ab%d" % s, bufs=2)
+                nc.sync.dma_start(out=st["ab", k, s][:], in_=view[:, rows(k), :])
+
         ident = const.tile([P, P], BF16, name="ident")
         make_identity(nc, ident[:])
         ident32 = const.tile([P, P], F32, name="ident32")
@@ -53,6 +77,7 @@ def tile_rwkv_timemix_for_quant_pa_t_kernel(
         nc.vector.memset(mixrows[:], 0.0)
         nc.sync.dma_start(out=mixrows[0:2, :], in_=time_mix_k.rearrange("o (u w) -> (o u) w", u=2))
         nc.sync.dma_start(out=mixrows[2:4, :], in_=time_mix_v.rearrange("o (u w) -> (o u) w", u=2))
+        load_mixing(0)
         vecs = const.tile([P, P], BF16, name="vecs")
         nc.vector.memset(vecs[:], 0.0)
         nc.sync.dma_start(out=vecs[0:2, :], in_=time_first.rearrange("(h p) -> h p", p=P))
@@ -63,9 +88,9 @@ def tile_rwkv_timemix_for_quant_pa_t_kernel(
             nc.sync.dma_start(out=wt[:], in_=w.rearrange("(h p) k -> p h k", p=P))
             w_sb.append(wt)
 
-        mix_t = psum.tile([P, P], F32, name="mix_t", tag="xT", bufs=2)
+        mix_t = psum.tile([P, P], F32, name="mix_t", tag="X", bufs=2)
         nc.tensor.transpose(mix_t[:], mixrows[:].bitcast(F32), ident32[:])
-        vecs_t = psum.tile([P, P], BF16, name="vecs_t", tag="xT", bufs=2)
+        vecs_t = psum.tile([P, P], BF16, name="vecs_t", tag="X", bufs=2)
         nc.tensor.transpose(vecs_t[:], vecs[:], ident[:])
         cst = const.tile([P, 12], F32, name="cst")
         nc.vector.tensor_copy(out=cst[:, 0:8], in_=mix_t[:].bitcast(BF16)[:, 0:8])
@@ -82,11 +107,20 @@ def tile_rwkv_timemix_for_quant_pa_t_kernel(
         nc.vector.memset(c1t[:], 0.0)
         for h in range(NH):
             nc.vector.tensor_scalar(out=c1t[:, h, :], in0=c1t[:, h, :], scalar1=c1[:, h:h + 1], scalar2=None, op0=ALU.add)
+        one = const.tile([P, P], F32, name="one")
+        nc.vector.memset(one[:], 1.0)
+        ec1 = const.tile([P, NH], F32, name="ec1")
+        nc.scalar.activation(out=ec1[:], in_=c1[:], func=ACT.Exp)
+        c1p = const.tile([P, NH], F32, name="c1p")
+        nc.vector.tensor_scalar(out=c1p[:], in0=c1[:], scalar1=0.0, scalar2=-1.0, op0=ALU.max, op1=ALU.mult)
+        top = const.tile([P, NH], F32, name="top")
+        nc.vector.tensor_scalar(out=top[:], in0=c1p[:], scalar1=EXP_TOP, scalar2=None, op0=ALU.add)
 
-        w_codes = []
-        w_scales = []
-        for wi in range(2):
-            w_t = psum.tile([P, 2, D], F32, name="w_t%d" % wi, tag="sxT", bufs=2)
+        w_codes = [None, None]
+        w_scales = [None, None]
+
+        def prepare_weights(wi):
+            w_t = psum.tile([P, 2, D], F32, name="w_t%d" % wi, tag="N", bufs=3)
             for h in range(NH):
                 for u in range(2):
                     nc.tensor.transpose(
@@ -98,40 +132,37 @@ def tile_rwkv_timemix_for_quant_pa_t_kernel(
             wc = const.tile([P, D], U32, name="wc%d" % wi, align_bytes=64)
             ws = const.tile([P, D], U8, name="ws%d" % wi, align_bytes=64)
             nc.vector.quantize_mx(out=wc[:].bitcast(FP8X4), scales=ws[:], in_=wg[:].rearrange("p d t -> p (d t)"))
-            w_codes.append(wc)
-            w_scales.append(ws)
+            w_codes[wi] = wc
+            w_scales[wi] = ws
 
-        st = {}
-
-        def live(k):
-            return 0 <= k < NB
-
-        def rows(k):
-            return slice(k * JB, (k + 1) * JB)
-
-        def load_front(k):
-            st["x", k] = loads.tile([P, JB, E], BF16, name="x_sb")
-            nc.sync.dma_start(out=st["x", k][:], in_=x_v[:, rows(k), :])
-            st["sx", k] = loads.tile([P, JB, E], BF16, name="sx_sb")
-            nc.sync.dma_start(out=st["sx", k][:], in_=sx_v[:, rows(k), :])
-            st["sp", k] = loads.tile([P, JB, D], BF16, name="sp_sb", bufs=2)
-            nc.sync.dma_start(out=st["sp", k][:], in_=sp_v[:, rows(k), :])
-
-        def load_states(k):
-            st["sab", k] = loads.tile([P, 2, JB, D], BF16, name="sab", bufs=2)
-            nc.sync.dma_start(out=st["sab", k][:, 0, :, :], in_=sa_v[:, rows(k), :])
-            nc.sync.dma_start(out=st["sab", k][:, 1, :, :], in_=sb_v[:, rows(k), :])
+        def words_back(k, u, key, src, tag, bufs):
+            st[key, k, u] = psum.tile([P, R], F32, name=key, tag=tag, bufs=bufs)
+            for jj in range(JB):
+                nc.tensor.transpose(
+                    st[key, k, u][:, jj * P:(jj + 1) * P], st[src, k][:, jj, :].bitcast(F32)[:, u * P:(u + 1) * P],
+                    ident32[:])
 
         def transpose_x(k, u):
-            st["sxT", k, u] = psum.tile([P, R], F32, name="sxT", tag="sxT", bufs=2)
-            st["xT", k, u] = psum.tile([P, R], F32, name="xT", tag="xT", bufs=2)
-            for key, src in (("sxT", "sx"), ("xT", "x")):
-                for jj in range(JB):
-                    nc.tensor.transpose(
-                        st[key, k, u][:, jj * P:(jj + 1) * P], st[src, k][:, jj, :].bitcast(F32)[:, u * P:(u + 1) * P],
-                        ident32[:])
+            words_back(k, u, "xT", "x", "X", 2)
+
+        def transpose_sx(k, u):
+            words_back(k, u, "sxT", "sx", "T", 2)
+
+        def sx_words(k, u):
+            st["sxw", k, u] = work.tile([P, R], F32, name="sxw")
+            nc.scalar.copy(out=st["sxw", k, u][:], in_=st["sxT", k, u][:])
 
         def products(k, u):
+            pair = st["sxw", k, u][:].bitcast(BF16).rearrange("p (r e) -> p r e", e=2)
+            for m in range(2):
+                st["prod", k, u, m] = work.tile([P, 2, R], F32, name="prod%d" % m)
+                for e in range(2):
+                    c = 4 * m + 2 * u + e
+                    nc.gpsimd.tensor_scalar(
+                        out=st["prod", k, u, m][:, e, :], in0=pair[:, :, e], scalar1=omix[:, c:c + 1], scalar2=0.0,
+                        op0=ALU.mult, op1=ALU.add)
+
+        def products_scalar(k, u):
             pair = st["sxT", k, u][:].bitcast(BF16).rearrange("p (r e) -> p r e", e=2)
             for m in range(2):
                 st["prod", k, u, m] = work.tile([P, 2, R], F32, name="prod%d" % m)
@@ -153,12 +184,11 @@ def tile_rwkv_timemix_for_quant_pa_t_kernel(
                         out=st["plane", k, m][:, t, :], in0=pair[:, :, e], scalar=cst[:, c:c + 1],
                         in1=st["prod", k, u, m][:, e, :], op0=ALU.mult, op1=ALU.add)
 
-        def regroup(k):
-            for m in range(2):
-                st["grouped", k, m] = single.tile([P, R, PACK], BF16, name="grouped%d" % m, align_bytes=64)
-                nc.scalar.copy(
-                    out=st["grouped", k, m][:].rearrange("p (c i) t -> p c t i", i=4),
-                    in_=st["plane", k, m][:].rearrange("p t (c i) -> p c t i", i=4))
+        def regroup(k, m, copy=nc.scalar.copy):
+            st["grouped", k, m] = single.tile([P, R, PACK], BF16, name="grouped%d" % m, align_bytes=64)
+            copy(
+                out=st["grouped", k, m][:].rearrange("p (c i) t -> p c t i", i=4),
+                in_=st["plane", k, m][:].rearrange("p t (c i) -> p c t i", i=4))
 
         def quantise(k, m):
             st["cd", k, m] = work.tile([P, R], U32, name="cd%d" % m, align_bytes=64)
@@ -167,171 +197,301 @@ def tile_rwkv_timemix_for_quant_pa_t_kernel(
                 out=st["cd", k, m][:].bitcast(FP8X4), scales=st["sc", k, m][:],
                 in_=st["grouped", k, m][:].rearrange("p r t -> p (r t)"))
 
-        def transpose_sp(k):
-            st["spT", k] = psum.tile([P, NH, R], BF16, name="spT", tag="sxT", bufs=2)
+        def project(k, m, h):
+            hs = slice(h * P, (h + 1) * P)
+            st["ps", k, m, h] = psum.tile([P, R], F32, name="ps", tag="T", bufs=2)
+            nc.tensor.matmul_mx(
+                out=st["ps", k, m, h][:], lhsT=w_codes[m][:, hs].bitcast(FP8X4), lhsT_scale=w_scales[m][:, hs],
+                rhs=st["cd", k, m][:].bitcast(FP8X4), rhs_scale=st["sc", k, m][:], start=True, stop=True)
+
+        def copy_out(k, m, h):
+            if h == 0:
+                st["kv"[m], k] = work.tile([P, NH, R], F32, name="kv"[m])
+            nc.scalar.copy(out=st["kv"[m], k][:, h, :], in_=st["ps", k, m, h][:])
+
+        def states_back(k, key, src, tag, bufs):
+            st[key, k] = psum.tile([P, NH, R], BF16, name=key, tag=tag, bufs=bufs)
             for h in range(NH):
                 for jj in range(JB):
                     nc.tensor.transpose(
-                        st["spT", k][:, h, jj * P:(jj + 1) * P], st["sp", k][:, jj, h * P:(h + 1) * P], ident[:])
+                        st[key, k][:, h, jj * P:(jj + 1) * P], st[src][:, jj, h * P:(h + 1) * P], ident[:])
 
-        def shift_sp(k):
-            st["q2", k] = work.tile([P, NH, R], F32, name="q2")
+        def transpose_sp(k):
+            states_back(k, "spT", ("sp", k), "K", 1)
+
+        def difference(k):
+            st["d2", k] = single.tile([P, NH, R], F32, name="d2")
             for h in range(NH):
-                nc.scalar.activation(
-                    out=st["q2", k][:, h, :], in_=st["spT", k][:, h, :], func=ACT.Identity, bias=td[:, h:h + 1])
+                nc.vector.scalar_tensor_tensor(
+                    out=st["d2", k][:, h, :], in0=st["spT", k][:, h, :], scalar=td[:, h:h + 1], in1=st["k", k][:, h, :],
+                    op0=ALU.add, op1=ALU.subtract)
 
-        def key_pass(k, h):
-            hs = slice(h * P, (h + 1) * P)
-            st["k_ps", k, h] = psum.tile([P, R], F32, name="k_ps", tag="kp")
-            nc.tensor.matmul_mx(
-                out=st["k_ps", k, h][:], lhsT=w_codes[0][:, hs].bitcast(FP8X4), lhsT_scale=w_scales[0][:, hs],
-                rhs=st["cd", k, 0][:].bitcast(FP8X4), rhs_scale=st["sc", k, 0][:], start=True, stop=True)
-
-        def difference(k, h):
-            if h == 0:
-                st["d2", k] = work.tile([P, NH, R], F32, name="d2")
-            nc.vector.tensor_tensor(
-                out=st["d2", k][:, h, :], in0=st["q2", k][:, h, :], in1=st["k_ps", k, h][:], op=ALU.subtract)
+        def clamp(k):
+            st["dc", k] = work.tile([P, NH, R], F32, name="dc")
+            for h in range(NH):
+                nc.gpsimd.tensor_scalar(
+                    out=st["dc", k][:, h, :], in0=st["d2", k][:, h, :], scalar1=top[:, h:h + 1], scalar2=0.0,
+                    op0=ALU.min, op1=ALU.add)
 
         def relu_part(k):
-            st["r2", k] = single.tile([P, NH, R], F32, name="r2")
-            nc.scalar.activation(out=st["r2", k][:], in_=st["d2", k][:], func=ACT.Relu, scale=-1.0)
+            st["r2", k] = work.tile([P, NH, R], F32, name="r2")
+            nc.gpsimd.tensor_scalar(
+                out=st["r2", k][:], in0=st["d2", k][:], scalar1=0.0, scalar2=0.0, op0=ALU.max, op1=ALU.add)
+
+        def grow(k):
+            st["ep", k] = single.tile([P, NH, R], F32, name="ep")
+            nc.scalar.activation(out=st["ep", k][:], in_=st["dc", k][:], func=ACT.Exp)
+
+        def transpose_state(k, s):
+            states_back(k, "abT%d" % s, ("ab", k, s), "K", 1)
+
+        def state_product(k, s):
+            st["g", k, s] = work.tile([P, NH, R], F32, name="g%d" % s)
+            nc.vector.tensor_tensor(
+                out=st["g", k, s][:], in0=st["ep", k][:], in1=st["abT%d" % s, k][:], op=ALU.mult)
+
+        def scaled_products(k, s):
+            st["cg", k, s] = work.tile([P, NH, R], F32, name="cg%d" % s)
+            for h in range(NH):
+                nc.gpsimd.tensor_scalar(
+                    out=st["cg", k, s][:, h, :], in0=st["g", k, s][:, h, :], scalar1=ec1[:, h:h + 1],
+                    scalar2=float(s), op0=ALU.mult, op1=ALU.add)
 
         def cols_of(pr, j2):
             return slice((2 * pr + j2) * P, (2 * pr + j2 + 1) * P)
 
-        def arguments_back(k, pr):
-            st["dl2", k, pr] = psum.tile([P, 2, D], F32, name="dl2")
-            st["dl1", k, pr] = psum.tile([P, 2, D], F32, name="dl1")
+        def back(k, pr, key, parts, tag="N", bufs=3):
+            st[key, k, pr] = psum.tile([P, 2, D], F32, name=key, tag=tag, bufs=bufs)
             for j2 in range(2):
                 for h in range(NH):
-                    nc.tensor.transpose(
-                        st["dl2", k, pr][:, j2, h * P:(h + 1) * P], st["d2", k][:, h, cols_of(pr, j2)], ident32[:])
-            for j2 in range(2):
-                for h in range(NH):
-                    hs = slice(h * P, (h + 1) * P)
-                    nc.tensor.matmul(
-                        out=st["dl1", k, pr][:, j2, hs], lhsT=st["d2", k][:, h, cols_of(pr, j2)], rhs=ident32[:],
-                        is_transpose=True, start=True, stop=False)
-                    nc.tensor.matmul(
-                        out=st["dl1", k, pr][:, j2, hs], lhsT=c1t[:, h, :], rhs=ident32[:],
-                        is_transpose=True, start=False, stop=True)
+                    for n, part in enumerate(parts):
+                        nc.tensor.matmul(
+                            out=st[key, k, pr][:, j2, h * P:(h + 1) * P],
+                            lhsT=c1t[:, h, :] if part == "c1" else one[:] if part == "one" else st[part][:, h, cols_of(pr, j2)],
+                            rhs=ident32[:], is_transpose=True, start=n == 0, stop=n == len(parts) - 1)
+
+        def arguments_back(k, pr, half):
+            place = ("X", 2) if k == NB - 1 or k == NB - 2 and pr == 1 else ("N", 3)
+            back(k, pr, "dl%d" % half, [("dc", k)] if half == 1 else [("dc", k), "c1"], *place)
+
+        def shrink(k, pr, half):
+            if pr == 0:
+                st["em", k, half] = work.tile([P, JB, D], F32, name="em%d" % half)
+            nc.scalar.activation(
+                out=st["em", k, half][:, 2 * pr:2 * pr + 2, :], in_=st["dl%d" % half, k, pr][:], func=ACT.Exp, scale=-1.0)
+
+        def open_outputs(k):
+            for i in range(5):
+                st["o", k, i] = outs.tile([P, JB, D], F32, name="o%d" % i)
 
         def new_p_back(k, pr):
-            st["po", k, pr] = psum.tile([P, 2, D], F32, name="po", tag="kp")
-            for j2 in range(2):
-                for h in range(NH):
-                    hs = slice(h * P, (h + 1) * P)
-                    nc.tensor.matmul(
-                        out=st["po", k, pr][:, j2, hs], lhsT=st["q2", k][:, h, cols_of(pr, j2)], rhs=ident32[:],
-                        is_transpose=True, start=True, stop=False)
-                    nc.tensor.matmul(
-                        out=st["po", k, pr][:, j2, hs], lhsT=st["r2", k][:, h, cols_of(pr, j2)], rhs=ident32[:],
-                        is_transpose=True, start=False, stop=True)
+            place = ("T", 2) if k == NB - 1 else ("X", 2) if k == NB - 2 else ("N", 3)
+            back(k, pr, "po", [("k", k), ("r2", k)], *place)
 
-        def value_pass(k, pr):
-            st["v_ps", k, pr] = psum.tile([P, 2, D], F32, name="v_ps")
-            for j2 in range(2):
-                cols = cols_of(pr, j2)
-                nc.tensor.matmul_mx(
-                    out=st["v_ps", k, pr][:, j2, :], lhsT=st["cd", k, 1][:, cols].bitcast(FP8X4),
-                    lhsT_scale=st["sc", k, 1][:, cols], rhs=w_codes[1][:].bitcast(FP8X4), rhs_scale=w_scales[1][:],
-                    start=True, stop=True)
+        def new_p(k, pr):
+            nc.scalar.copy(out=st["o", k, 4][:, 2 * pr:2 * pr + 2, :], in_=st["po", k, pr][:])
 
-        def exponentials(k, pr):
-            ps = slice(2 * pr, 2 * pr + 2)
-            if pr == 0:
-                for half in range(2):
-                    st["ep", k, half] = work.tile([P, JB, D], F32, name="ep%d" % half)
-                    st["em", k, half] = work.tile([P, JB, D], F32, name="em%d" % half)
-                for i in range(5):
-                    st["o", k, i] = outs.tile([P, JB, D], F32, name="o%d" % i)
-            for half, key in ((1, "dl2"), (0, "dl1")):
-                nc.scalar.activation(out=st["em", k, half][:, ps, :], in_=st[key, k, pr][:], func=ACT.Exp, scale=-1.0)
-                nc.scalar.activation(out=st["ep", k, half][:, ps, :], in_=st[key, k, pr][:], func=ACT.Exp)
-            nc.scalar.copy(out=st["o", k, 4][:, ps, :], in_=st["po", k, pr][:])
+        def sum_back(k, pr, i):
+            parts = {0: [("cg", k, 0), ("v", k)], 1: [("cg", k, 1)], 2: [("g", k, 0), ("v", k)], 3: [("g", k, 1), "one"]}[i]
+            back(k, pr, "sum%d" % i, parts)
 
-        def value_products(k, pr):
-            ps = slice(2 * pr, 2 * pr + 2)
-            for half in (1, 0):
-                if pr == 0:
-                    st["t2", k, half] = single.tile([P, JB, D], F32, name="t2_%d" % half)
-                nc.vector.scalar_tensor_tensor(
-                    out=st["t2", k, half][:, ps, :], in0=st["em", k, half][:, ps, :], scalar=1.0,
-                    in1=st["v_ps", k, pr][:], op0=ALU.min, op1=ALU.mult)
-
-        def state_products(k, half):
-            st["t13", k, half] = single.tile([P, 2, JB * D], F32, name="t13_%d" % half)
+        def output(k, pr, i):
+            half, s = divmod(i, 2)
+            out = st["o", k, i][:, 2 * pr:2 * pr + 2, :]
+            em = st["em", k, half][:, 2 * pr:2 * pr + 2, :]
             nc.vector.scalar_tensor_tensor(
-                out=st["t13", k, half][:],
-                in0=st["ep", k, half][:].rearrange("p j d -> p (j d)").unsqueeze(1).to_broadcast([P, 2, JB * D]),
-                scalar=1.0, in1=st["sab", k][:].rearrange("p s j d -> p s (j d)"), op0=ALU.min, op1=ALU.mult)
+                out=out, in0=em, scalar=1.0, in1=st["sum%d" % i, k, pr][:], op0=ALU.min, op1=ALU.mult)
 
-        def sum_b(k, half):
-            nc.vector.scalar_tensor_tensor(
-                out=st["o", k, 2 * half + 1][:].rearrange("p j d -> p (j d)"),
-                in0=st["em", k, half][:].rearrange("p j d -> p (j d)"), scalar=1.0, in1=st["t13", k, half][:, 1, :],
-                op0=ALU.min, op1=ALU.add)
-
-        def sum_a(k, half):
-            nc.vector.tensor_tensor(
-                out=st["o", k, 2 * half][:].rearrange("p j d -> p (j d)"), in0=st["t13", k, half][:, 0, :],
-                in1=st["t2", k, half][:].rearrange("p j d -> p (j d)"), op=ALU.add)
-
-        def store(k):
-            for i in (4, 3, 2, 1, 0):
-                nc.sync.dma_start(out=out_v[i][:, rows(k), :], in_=st["o", k, i][:])
+        def store(k, i):
+            nc.sync.dma_start(out=out_v[i][:, rows(k), :], in_=st["o", k, i][:])
 
         with tc.manual_schedule():
-            for i in range(-3, NB + 1):
-                prev, cur, nxt, nx2 = i - 1, i, i + 1, i + 2
-                if live(i + 3):
-                    load_front(i + 3)
-                if live(nxt):
-                    load_states(nxt)
-                    transpose_x(nxt, 1)
-                    products(nxt, 0)
-                if live(cur):
-                    relu_part(cur)
-                    new_p_back(cur, 0)
-                if live(nxt):
-                    mix(nxt, 0)
-                if live(nx2):
-                    transpose_sp(nx2)
-                if live(prev):
-                    sum_a(prev, 1)
-                    sum_b(prev, 0)
-                    sum_a(prev, 0)
-                    store(prev)
-                if live(cur):
-                    exponentials(cur, 0)
-                    value_products(cur, 0)
-                    arguments_back(cur, 1)
-                    value_pass(cur, 1)
-                    new_p_back(cur, 1)
-                if live(nxt):
-                    products(nxt, 1)
-                    mix(nxt, 1)
-                if live(nx2):
-                    transpose_x(nx2, 0)
-                if live(cur):
-                    exponentials(cur, 1)
-                    value_products(cur, 1)
-                    state_products(cur, 1)
-                    state_products(cur, 0)
-                if live(nxt):
-                    regroup(nxt)
-                    quantise(nxt, 0)
-                    key_pass(nxt, 0)
-                if live(cur):
-                    sum_b(cur, 1)
-                if live(nxt):
-                    difference(nxt, 0)
-                    quantise(nxt, 1)
-                    key_pass(nxt, 1)
-                    value_pass(nxt, 0)
-                    difference(nxt, 1)
-                if live(nx2):
-                    shift_sp(nx2)
-                if live(nxt):
-                    arguments_back(nxt, 0)
+            for i in range(-3, NB - 1):
+                c, b, a, a1, ld = i - 1, i, i + 1, i + 2, i + 3
+                if live(ld):
+                    if ld > 0:
+                        load_mixing(ld)
+                    load_sp(ld)
+                if live(a):
+                    load_states(a)
+                if live(b):
+                    quantise(b, 0)
+                    quantise(b, 1)
+                if live(c):
+                    open_outputs(c)
+                    scaled_products(c, 1)
+                    shrink(c, 0, 1)
+                if live(b):
+                    project(b, 0, 0)
+                    project(b, 0, 1)
+                    copy_out(b, 0, 0)
+                    copy_out(b, 0, 1)
+                    transpose_sp(b)
+                if live(c):
+                    shrink(c, 0, 0)
+                    arguments_back(c, 1, 1)
+                    arguments_back(c, 1, 0)
+                    shrink(c, 1, 1)
+                    shrink(c, 1, 0)
+                if live(a):
+                    if a > 0:
+                        products(a, 1)
+                    mix(a, 0)
+                if live(b):
+                    project(b, 1, 0)
+                    copy_out(b, 1, 0)
+                    project(b, 1, 1)
+                    copy_out(b, 1, 1)
+                    difference(b)
+                    clamp(b)
+                if live(c):
+                    new_p_back(c, 0)
+                    new_p(c, 0)
+                    new_p_back(c, 1)
+                    new_p(c, 1)
+                    store(c, 4)
+                    sum_back(c, 0, 3)
+                if live(a1):
+                    transpose_x(a1, 0)
+                    transpose_sx(a1, 0)
+                    sx_words(a1, 0)
+                    products(a1, 0)
+                if live(b):
+                    grow(b)
+                    relu_part(b)
+                if live(c):
+                    sum_back(c, 0, 2)
+                if live(a):
+                    mix(a, 1)
+                if live(c):
+                    sum_back(c, 0, 1)
+                if live(a):
+                    regroup(a, 0)
+                    regroup(a, 1, nc.scalar.copy if a > 0 else nc.vector.tensor_copy)
+                    if a == 0:
+                        prepare_weights(0)
+                        prepare_weights(1)
+                if live(c):
+                    output(c, 0, 3)
+                    output(c, 0, 2)
+                    output(c, 0, 1)
+                    sum_back(c, 0, 0)
+                    output(c, 0, 0)
+                if live(b):
+                    transpose_state(b, 0)
+                    state_product(b, 0)
+                    scaled_products(b, 0)
+                if live(a1):
+                    transpose_x(a1, 1)
+                if live(c):
+                    for o in (3,2):
+                        sum_back(c, 1, o)
+                        output(c, 1, o)
+                        store(c, o)
+                if live(b):
+                    transpose_state(b, 1)
+                    state_product(b, 1)
+                if live(c):
+                    for o in (1,0):
+                        sum_back(c, 1, o)
+                        output(c, 1, o)
+                        store(c, o)
+                if live(a1):
+                    transpose_sx(a1, 1)
+                    if a1 > 0:
+                        sx_words(a1, 1)
+                    else:
+                        products_scalar(a1, 1)
+                if live(b):
+                    arguments_back(b, 0, 1)
+                    arguments_back(b, 0, 0)
+
+            b, c = NB - 1, NB - 2
+            open_outputs(c)
+            open_outputs(b)
+            quantise(b, 0)
+            quantise(b, 1)
+            scaled_products(c, 1)
+            shrink(c, 0, 1)
+            project(b, 0, 0)
+            project(b, 0, 1)
+            copy_out(b, 0, 0)
+            copy_out(b, 0, 1)
+            transpose_sp(b)
+            sum_back(c, 0, 3)
+            shrink(c, 0, 0)
+            arguments_back(c, 1, 1)
+            arguments_back(c, 1, 0)
+            shrink(c, 1, 1)
+            shrink(c, 1, 0)
+            output(c, 0, 3)
+            difference(b)
+            clamp(b)
+            relu_part(b)
+            sum_back(c, 0, 2)
+            output(c, 0, 2)
+            project(b, 1, 0)
+            project(b, 1, 1)
+            sum_back(c, 0, 1)
+            output(c, 0, 1)
+            new_p_back(c, 0)
+            new_p(c, 0)
+            new_p_back(c, 1)
+            new_p(c, 1)
+            store(c, 4)
+            sum_back(c, 0, 0)
+            output(c, 0, 0)
+            grow(b)
+            copy_out(b, 1, 0)
+            copy_out(b, 1, 1)
+            sum_back(c, 1, 3)
+            output(c, 1, 3)
+            store(c, 3)
+            transpose_state(b, 0)
+            state_product(b, 0)
+            scaled_products(b, 0)
+            sum_back(c, 1, 2)
+            output(c, 1, 2)
+            store(c, 2)
+            arguments_back(b, 0, 1)
+            arguments_back(b, 0, 0)
+            shrink(b, 0, 1)
+            shrink(b, 0, 0)
+            transpose_state(b, 1)
+            sum_back(c, 1, 1)
+            output(c, 1, 1)
+            store(c, 1)
+            state_product(b, 1)
+            scaled_products(b, 1)
+            arguments_back(b, 1, 1)
+            arguments_back(b, 1, 0)
+            shrink(b, 1, 1)
+            shrink(b, 1, 0)
+            sum_back(c, 1, 0)
+            output(c, 1, 0)
+            store(c, 0)
+            sum_back(b, 0, 2)
+            output(b, 0, 2)
+            sum_back(b, 0, 3)
+            output(b, 0, 3)
+            new_p_back(b, 0)
+            new_p(b, 0)
+            new_p_back(b, 1)
+            new_p(b, 1)
+            store(b, 4)
+            sum_back(b, 1, 2)
+            output(b, 1, 2)
+            store(b, 2)
+            sum_back(b, 1, 3)
+            output(b, 1, 3)
+            store(b, 3)
+            sum_back(b, 0, 0)
+            output(b, 0, 0)
+            sum_back(b, 1, 0)
+            output(b, 1, 0)
+            store(b, 0)
+            sum_back(b, 0, 1)
+            output(b, 0, 1)
+            sum_back(b, 1, 1)
+            output(b, 1, 1)
+            store(b, 1)

@@ -229,14 +229,13 @@ def tile_rwkv_timemix_for_quant_pa_t_kernel(
         def clamp(k):
             st["dc", k] = work.tile([P, NH, R], F32, name="dc")
             for h in range(NH):
-                nc.gpsimd.tensor_scalar(
-                    out=st["dc", k][:, h, :], in0=st["d2", k][:, h, :], scalar1=top[:, h:h + 1], scalar2=0.0,
-                    op0=ALU.min, op1=ALU.add)
+                nc.vector.tensor_scalar(
+                    out=st["dc", k][:, h, :], in0=st["d2", k][:, h, :], scalar1=top[:, h:h + 1], scalar2=None,
+                    op0=ALU.min)
 
         def relu_part(k):
             st["r2", k] = work.tile([P, NH, R], F32, name="r2")
-            nc.gpsimd.tensor_scalar(
-                out=st["r2", k][:], in0=st["d2", k][:], scalar1=0.0, scalar2=0.0, op0=ALU.max, op1=ALU.add)
+            nc.scalar.activation(out=st["r2", k][:], in_=st["d2", k][:], func=ACT.Relu)
 
         def grow(k):
             st["ep", k] = single.tile([P, NH, R], F32, name="ep")

from contextlib import ExitStack

import concourse.mybir as mybir
from concourse.masks import make_identity

F32 = mybir.dt.float32
BF16 = mybir.dt.bfloat16
U32 = mybir.dt.uint32
U8 = mybir.dt.uint8
FP8X4 = mybir.dt.float8_e4m3fn_x4
ALU = mybir.AluOpType
ACT = mybir.ActivationFunctionType

P = 128
B = 4096
E = 512
D = 256
NJ = B // P
PACK = 4
JB = 4
NB = NJ // JB
R = JB * P
NH = D // P
EXP_TOP = 80.0
FLOPS = 2 * B * E * D * 2


def tile_rwkv_timemix_for_quant_pa_t_kernel(
    tc, x, state_A, state_B, state_p, state_x, time_decay, time_first,
    time_mix_k, time_mix_v, W_key, W_value, out_0, out_1, out_2, out_3, out_4,
):
    nc = tc.nc
    with ExitStack() as ctx:
        const = ctx.enter_context(tc.tile_pool(name="const", bufs=1))
        loads = ctx.enter_context(tc.tile_pool(name="loads", bufs=3))
        work = ctx.enter_context(tc.tile_pool(name="work", bufs=2))
        single = ctx.enter_context(tc.tile_pool(name="single", bufs=1))
        outs = ctx.enter_context(tc.tile_pool(name="outs", bufs=2))
        psum = ctx.enter_context(tc.psum_pool(name="psum", bufs=1))

        x_v = x.rearrange("(p j) k -> p j k", j=NJ)
        sx_v = state_x.rearrange("(p j) k -> p j k", j=NJ)
        sa_v = state_A.rearrange("(p j) d -> p j d", j=NJ)
        sb_v = state_B.rearrange("(p j) d -> p j d", j=NJ)
        sp_v = state_p.rearrange("(p j) d -> p j d", j=NJ)
        out_v = [o.rearrange("(p j) d -> p j d", j=NJ) for o in (out_0, out_1, out_2, out_3, out_4)]

        st = {}

        def live(k):
            return 0 <= k < NB

        def rows(k):
            return slice(k * JB, (k + 1) * JB)

        def load_mixing(k):
            st["sx", k] = loads.tile([P, JB, E], BF16, name="sx_sb")
            nc.sync.dma_start(out=st["sx", k][:], in_=sx_v[:, rows(k), :])
            st["x", k] = loads.tile([P, JB, E], BF16, name="x_sb")
            nc.sync.dma_start(out=st["x", k][:], in_=x_v[:, rows(k), :])

        def load_sp(k):
            st["sp", k] = loads.tile([P, JB, D], BF16, name="sp_sb", bufs=2)
            nc.sync.dma_start(out=st["sp", k][:], in_=sp_v[:, rows(k), :])

        def load_states(k):
            for s, view in enumerate((sa_v, sb_v)):
                st["ab", k, s] = loads.tile([P, JB, D], BF16, name="ab%d" % s, bufs=2)
                nc.sync.dma_start(out=st["ab", k, s][:], in_=view[:, rows(k), :])

        ident = const.tile([P, P], BF16, name="ident")
        make_identity(nc, ident[:])
        ident32 = const.tile([P, P], F32, name="ident32")
        make_identity(nc, ident32[:])

        mixrows = const.tile([P, 2 * P], BF16, name="mixrows")
        nc.vector.memset(mixrows[:], 0.0)
        nc.sync.dma_start(out=mixrows[0:2, :], in_=time_mix_k.rearrange("o (u w) -> (o u) w", u=2))
        nc.sync.dma_start(out=mixrows[2:4, :], in_=time_mix_v.rearrange("o (u w) -> (o u) w", u=2))
        load_mixing(0)
        vecs = const.tile([P, P], BF16, name="vecs")
        nc.vector.memset(vecs[:], 0.0)
        nc.sync.dma_start(out=vecs[0:2, :], in_=time_first.rearrange("(h p) -> h p", p=P))
        nc.sync.dma_start(out=vecs[2:4, :], in_=time_decay.rearrange("(h p) -> h p", p=P))
        w_sb = []
        for wi, w in enumerate((W_key, W_value)):
            wt = const.tile([P, NH, E], BF16, name="w_sb%d" % wi)
            nc.sync.dma_start(out=wt[:], in_=w.rearrange("(h p) k -> p h k", p=P))
            w_sb.append(wt)

        mix_t = psum.tile([P, P], F32, name="mix_t", tag="X", bufs=2)
        nc.tensor.transpose(mix_t[:], mixrows[:].bitcast(F32), ident32[:])
        vecs_t = psum.tile([P, P], BF16, name="vecs_t", tag="X", bufs=2)
        nc.tensor.transpose(vecs_t[:], vecs[:], ident[:])
        cst = const.tile([P, 12], F32, name="cst")
        nc.vector.tensor_copy(out=cst[:, 0:8], in_=mix_t[:].bitcast(BF16)[:, 0:8])
        nc.vector.tensor_copy(out=cst[:, 8:12], in_=vecs_t[:, 0:4])
        omix = const.tile([P, 8], F32, name="omix")
        nc.vector.tensor_scalar(out=omix[:], in0=cst[:, 0:8], scalar1=-1.0, scalar2=1.0, op0=ALU.mult, op1=ALU.add)
        ed = const.tile([P, NH], F32, name="ed")
        nc.scalar.activation(out=ed[:], in_=cst[:, 10:12], func=ACT.Exp)
        td = const.tile([P, NH], F32, name="td")
        nc.vector.tensor_scalar(out=td[:], in0=ed[:], scalar1=-1.0, scalar2=None, op0=ALU.mult)
        c1 = const.tile([P, NH], F32, name="c1")
        nc.vector.tensor_tensor(out=c1[:], in0=ed[:], in1=cst[:, 8:10], op=ALU.subtract)
        c1t = const.tile([P, NH, P], F32, name="c1t")
        nc.vector.memset(c1t[:], 0.0)
        for h in range(NH):
            nc.vector.tensor_scalar(out=c1t[:, h, :], in0=c1t[:, h, :], scalar1=c1[:, h:h + 1], scalar2=None, op0=ALU.add)
        one = const.tile([P, P], F32, name="one")
        nc.vector.memset(one[:], 1.0)
        ec1 = const.tile([P, NH], F32, name="ec1")
        nc.scalar.activation(out=ec1[:], in_=c1[:], func=ACT.Exp)
        c1p = const.tile([P, NH], F32, name="c1p")
        nc.vector.tensor_scalar(out=c1p[:], in0=c1[:], scalar1=0.0, scalar2=-1.0, op0=ALU.max, op1=ALU.mult)
        top = const.tile([P, NH], F32, name="top")
        nc.vector.tensor_scalar(out=top[:], in0=c1p[:], scalar1=EXP_TOP, scalar2=None, op0=ALU.add)

        w_codes = [None, None]
        w_scales = [None, None]

        def prepare_weights(wi):
            w_t = psum.tile([P, 2, D], F32, name="w_t%d" % wi, tag="N", bufs=3)
            for h in range(NH):
                for u in range(2):
                    nc.tensor.transpose(
                        w_t[:, u, h * P:(h + 1) * P], w_sb[wi][:, h, :].bitcast(F32)[:, u * P:(u + 1) * P], ident32[:])
            wg = const.tile([P, D, PACK], BF16, name="wg%d" % wi, align_bytes=64)
            nc.vector.tensor_copy(
                out=wg[:].rearrange("p d t -> p (d t)").bitcast(F32).rearrange("p (d u) -> p d u", u=2),
                in_=w_t[:].rearrange("p u d -> p d u"))
            wc = const.tile([P, D], U32, name="wc%d" % wi, align_bytes=64)
            ws = const.tile([P, D], U8, name="ws%d" % wi, align_bytes=64)
            nc.vector.quantize_mx(out=wc[:].bitcast(FP8X4), scales=ws[:], in_=wg[:].rearrange("p d t -> p (d t)"))
            w_codes[wi] = wc
            w_scales[wi] = ws

        def words_back(k, u, key, src, tag, bufs):
            st[key, k, u] = psum.tile([P, R], F32, name=key, tag=tag, bufs=bufs)
            for jj in range(JB):
                nc.tensor.transpose(
                    st[key, k, u][:, jj * P:(jj + 1) * P], st[src, k][:, jj, :].bitcast(F32)[:, u * P:(u + 1) * P],
                    ident32[:])

        def transpose_x(k, u):
            words_back(k, u, "xT", "x", "X", 2)

        def transpose_sx(k, u):
            words_back(k, u, "sxT", "sx", "T", 2)

        def sx_words(k, u):
            st["sxw", k, u] = work.tile([P, R], F32, name="sxw")
            nc.scalar.copy(out=st["sxw", k, u][:], in_=st["sxT", k, u][:])

        def products(k, u):
            pair = st["sxw", k, u][:].bitcast(BF16).rearrange("p (r e) -> p r e", e=2)
            for m in range(2):
                st["prod", k, u, m] = work.tile([P, 2, R], F32, name="prod%d" % m)
                for e in range(2):
                    c = 4 * m + 2 * u + e
                    nc.gpsimd.tensor_scalar(
                        out=st["prod", k, u, m][:, e, :], in0=pair[:, :, e], scalar1=omix[:, c:c + 1], scalar2=0.0,
                        op0=ALU.mult, op1=ALU.add)

        def products_scalar(k, u):
            pair = st["sxT", k, u][:].bitcast(BF16).rearrange("p (r e) -> p r e", e=2)
            for m in range(2):
                st["prod", k, u, m] = work.tile([P, 2, R], F32, name="prod%d" % m)
                for e in range(2):
                    c = 4 * m + 2 * u + e
                    nc.scalar.activation(
                        out=st["prod", k, u, m][:, e, :], in_=pair[:, :, e], func=ACT.Copy, scale=omix[:, c:c + 1])

        def mix(k, u):
            if u == 0:
                for m in range(2):
                    st["plane", k, m] = single.tile([P, PACK, R], BF16, name="plane%d" % m)
            pair = st["xT", k, u][:].bitcast(BF16).rearrange("p (r e) -> p r e", e=2)
            for m in range(2):
                for e in range(2):
                    t = 2 * u + e
                    c = 4 * m + t
                    nc.vector.scalar_tensor_tensor(
                        out=st["plane", k, m][:, t, :], in0=pair[:, :, e], scalar=cst[:, c:c + 1],
                        in1=st["prod", k, u, m][:, e, :], op0=ALU.mult, op1=ALU.add)

        def regroup(k, m, copy=nc.scalar.copy):
            st["grouped", k, m] = single.tile([P, R, PACK], BF16, name="grouped%d" % m, align_bytes=64)
            copy(
                out=st["grouped", k, m][:].rearrange("p (c i) t -> p c t i", i=4),
                in_=st["plane", k, m][:].rearrange("p t (c i) -> p c t i", i=4))

        def quantise(k, m):
            st["cd", k, m] = work.tile([P, R], U32, name="cd%d" % m, align_bytes=64)
            st["sc", k, m] = work.tile([P, R], U8, name="sc%d" % m, align_bytes=64)
            nc.vector.quantize_mx(
                out=st["cd", k, m][:].bitcast(FP8X4), scales=st["sc", k, m][:],
                in_=st["grouped", k, m][:].rearrange("p r t -> p (r t)"))

        def project(k, m, h):
            hs = slice(h * P, (h + 1) * P)
            st["ps", k, m, h] = psum.tile([P, R], F32, name="ps", tag="T", bufs=2)
            nc.tensor.matmul_mx(
                out=st["ps", k, m, h][:], lhsT=w_codes[m][:, hs].bitcast(FP8X4), lhsT_scale=w_scales[m][:, hs],
                rhs=st["cd", k, m][:].bitcast(FP8X4), rhs_scale=st["sc", k, m][:], start=True, stop=True)

        def copy_out(k, m, h):
            if h == 0:
                st["kv"[m], k] = work.tile([P, NH, R], F32, name="kv"[m])
            nc.scalar.copy(out=st["kv"[m], k][:, h, :], in_=st["ps", k, m, h][:])

        def states_back(k, key, src, tag, bufs):
            st[key, k] = psum.tile([P, NH, R], BF16, name=key, tag=tag, bufs=bufs)
            for h in range(NH):
                for jj in range(JB):
                    nc.tensor.transpose(
                        st[key, k][:, h, jj * P:(jj + 1) * P], st[src][:, jj, h * P:(h + 1) * P], ident[:])

        def transpose_sp(k):
            states_back(k, "spT", ("sp", k), "K", 1)

        def difference(k):
            st["d2", k] = single.tile([P, NH, R], F32, name="d2")
            for h in range(NH):
                nc.vector.scalar_tensor_tensor(
                    out=st["d2", k][:, h, :], in0=st["spT", k][:, h, :], scalar=td[:, h:h + 1], in1=st["k", k][:, h, :],
                    op0=ALU.add, op1=ALU.subtract)

        def clamp(k):
            st["dc", k] = work.tile([P, NH, R], F32, name="dc")
            for h in range(NH):
                nc.vector.tensor_scalar(
                    out=st["dc", k][:, h, :], in0=st["d2", k][:, h, :], scalar1=top[:, h:h + 1], scalar2=None,
                    op0=ALU.min)

        def relu_part(k):
            st["r2", k] = work.tile([P, NH, R], F32, name="r2")
            nc.scalar.activation(out=st["r2", k][:], in_=st["d2", k][:], func=ACT.Relu)

        def grow(k):
            st["ep", k] = single.tile([P, NH, R], F32, name="ep")
            nc.scalar.activation(out=st["ep", k][:], in_=st["dc", k][:], func=ACT.Exp)

        def transpose_state(k, s):
            states_back(k, "abT%d" % s, ("ab", k, s), "K", 1)

        def state_product(k, s):
            st["g", k, s] = work.tile([P, NH, R], F32, name="g%d" % s)
            nc.vector.tensor_tensor(
                out=st["g", k, s][:], in0=st["ep", k][:], in1=st["abT%d" % s, k][:], op=ALU.mult)

        def scaled_products(k, s):
            st["cg", k, s] = work.tile([P, NH, R], F32, name="cg%d" % s)
            for h in range(NH):
                nc.gpsimd.tensor_scalar(
                    out=st["cg", k, s][:, h, :], in0=st["g", k, s][:, h, :], scalar1=ec1[:, h:h + 1],
                    scalar2=float(s), op0=ALU.mult, op1=ALU.add)

        def cols_of(pr, j2):
            return slice((2 * pr + j2) * P, (2 * pr + j2 + 1) * P)

        def back(k, pr, key, parts, tag="N", bufs=3):
            st[key, k, pr] = psum.tile([P, 2, D], F32, name=key, tag=tag, bufs=bufs)
            for j2 in range(2):
                for h in range(NH):
                    for n, part in enumerate(parts):
                        nc.tensor.matmul(
                            out=st[key, k, pr][:, j2, h * P:(h + 1) * P],
                            lhsT=c1t[:, h, :] if part == "c1" else one[:] if part == "one" else st[part][:, h, cols_of(pr, j2)],
                            rhs=ident32[:], is_transpose=True, start=n == 0, stop=n == len(parts) - 1)

        def arguments_back(k, pr, half):
            place = ("X", 2) if k == NB - 1 or k == NB - 2 and pr == 1 else ("N", 3)
            back(k, pr, "dl%d" % half, [("dc", k)] if half == 1 else [("dc", k), "c1"], *place)

        def shrink(k, pr, half):
            if pr == 0:
                st["em", k, half] = work.tile([P, JB, D], F32, name="em%d" % half)
            nc.scalar.activation(
                out=st["em", k, half][:, 2 * pr:2 * pr + 2, :], in_=st["dl%d" % half, k, pr][:], func=ACT.Exp, scale=-1.0)

        def open_outputs(k):
            for i in range(5):
                st["o", k, i] = outs.tile([P, JB, D], F32, name="o%d" % i)

        def new_p_back(k, pr):
            place = ("T", 2) if k == NB - 1 else ("X", 2) if k == NB - 2 else ("N", 3)
            back(k, pr, "po", [("k", k), ("r2", k)], *place)

        def new_p(k, pr):
            nc.scalar.copy(out=st["o", k, 4][:, 2 * pr:2 * pr + 2, :], in_=st["po", k, pr][:])

        def sum_back(k, pr, i):
            parts = {0: [("cg", k, 0), ("v", k)], 1: [("cg", k, 1)], 2: [("g", k, 0), ("v", k)], 3: [("g", k, 1), "one"]}[i]
            back(k, pr, "sum%d" % i, parts)

        def output(k, pr, i):
            half, s = divmod(i, 2)
            out = st["o", k, i][:, 2 * pr:2 * pr + 2, :]
            em = st["em", k, half][:, 2 * pr:2 * pr + 2, :]
            nc.vector.scalar_tensor_tensor(
                out=out, in0=em, scalar=1.0, in1=st["sum%d" % i, k, pr][:], op0=ALU.min, op1=ALU.mult)

        def store(k, i):
            nc.sync.dma_start(out=out_v[i][:, rows(k), :], in_=st["o", k, i][:])

        with tc.manual_schedule():
            for i in range(-3, NB - 1):
                c, b, a, a1, ld = i - 1, i, i + 1, i + 2, i + 3
                if live(ld):
                    if ld > 0:
                        load_mixing(ld)
                    load_sp(ld)
                if live(a):
                    load_states(a)
                if live(b):
                    quantise(b, 0)
                    quantise(b, 1)
                if live(c):
                    open_outputs(c)
                    scaled_products(c, 1)
                    shrink(c, 0, 1)
                if live(b):
                    project(b, 0, 0)
                    project(b, 0, 1)
                    copy_out(b, 0, 0)
                    copy_out(b, 0, 1)
                    transpose_sp(b)
                if live(c):
                    shrink(c, 0, 0)
                    arguments_back(c, 1, 1)
                    arguments_back(c, 1, 0)
                    shrink(c, 1, 1)
                    shrink(c, 1, 0)
                if live(a):
                    if a > 0:
                        products(a, 1)
                    mix(a, 0)
                if live(b):
                    project(b, 1, 0)
                    copy_out(b, 1, 0)
                    project(b, 1, 1)
                    copy_out(b, 1, 1)
                    difference(b)
                    clamp(b)
                if live(c):
                    new_p_back(c, 0)
                    new_p(c, 0)
                    new_p_back(c, 1)
                    new_p(c, 1)
                    store(c, 4)
                    sum_back(c, 0, 3)
                if live(a1):
                    transpose_x(a1, 0)
                    transpose_sx(a1, 0)
                    sx_words(a1, 0)
                    products(a1, 0)
                if live(b):
                    grow(b)
                    relu_part(b)
                if live(c):
                    sum_back(c, 0, 2)
                if live(a):
                    mix(a, 1)
                if live(c):
                    sum_back(c, 0, 1)
                if live(a):
                    regroup(a, 0)
                    regroup(a, 1, nc.scalar.copy if a > 0 else nc.vector.tensor_copy)
                    if a == 0:
                        prepare_weights(0)
                        prepare_weights(1)
                if live(c):
                    output(c, 0, 3)
                    output(c, 0, 2)
                    output(c, 0, 1)
                    sum_back(c, 0, 0)
                    output(c, 0, 0)
                if live(b):
                    transpose_state(b, 0)
                    state_product(b, 0)
                    scaled_products(b, 0)
                if live(a1):
                    transpose_x(a1, 1)
                if live(c):
                    for o in (3,2):
                        sum_back(c, 1, o)
                        output(c, 1, o)
                        store(c, o)
                if live(b):
                    transpose_state(b, 1)
                    state_product(b, 1)
                if live(c):
                    for o in (1,0):
                        sum_back(c, 1, o)
                        output(c, 1, o)
                        store(c, o)
                if live(a1):
                    transpose_sx(a1, 1)
                    if a1 > 0:
                        sx_words(a1, 1)
                    else:
                        products_scalar(a1, 1)
                if live(b):
                    arguments_back(b, 0, 1)
                    arguments_back(b, 0, 0)

            b, c = NB - 1, NB - 2
            open_outputs(c)
            open_outputs(b)
            quantise(b, 0)
            quantise(b, 1)
            scaled_products(c, 1)
            shrink(c, 0, 1)
            project(b, 0, 0)
            project(b, 0, 1)
            copy_out(b, 0, 0)
            copy_out(b, 0, 1)
            transpose_sp(b)
            sum_back(c, 0, 3)
            shrink(c, 0, 0)
            arguments_back(c, 1, 1)
            arguments_back(c, 1, 0)
            shrink(c, 1, 1)
            shrink(c, 1, 0)
            output(c, 0, 3)
            difference(b)
            clamp(b)
            relu_part(b)
            sum_back(c, 0, 2)
            output(c, 0, 2)
            project(b, 1, 0)
            project(b, 1, 1)
            sum_back(c, 0, 1)
            output(c, 0, 1)
            new_p_back(c, 0)
            new_p(c, 0)
            new_p_back(c, 1)
            new_p(c, 1)
            store(c, 4)
            sum_back(c, 0, 0)
            output(c, 0, 0)
            grow(b)
            copy_out(b, 1, 0)
            copy_out(b, 1, 1)
            sum_back(c, 1, 3)
            output(c, 1, 3)
            store(c, 3)
            transpose_state(b, 0)
            state_product(b, 0)
            scaled_products(b, 0)
            sum_back(c, 1, 2)
            output(c, 1, 2)
            store(c, 2)
            arguments_back(b, 0, 1)
            arguments_back(b, 0, 0)
            shrink(b, 0, 1)
            shrink(b, 0, 0)
            transpose_state(b, 1)
            sum_back(c, 1, 1)
            output(c, 1, 1)
            store(c, 1)
            state_product(b, 1)
            scaled_products(b, 1)
            arguments_back(b, 1, 1)
            arguments_back(b, 1, 0)
            shrink(b, 1, 1)
            shrink(b, 1, 0)
            sum_back(c, 1, 0)
            output(c, 1, 0)
            store(c, 0)
            sum_back(b, 0, 2)
            output(b, 0, 2)
            sum_back(b, 0, 3)
            output(b, 0, 3)
            new_p_back(b, 0)
            new_p(b, 0)
            new_p_back(b, 1)
            new_p(b, 1)
            store(b, 4)
            sum_back(b, 1, 2)
            output(b, 1, 2)
            store(b, 2)
            sum_back(b, 1, 3)
            output(b, 1, 3)
            store(b, 3)
            sum_back(b, 0, 0)
            output(b, 0, 0)
            sum_back(b, 1, 0)
            output(b, 1, 0)
            store(b, 0)
            sum_back(b, 0, 1)
            output(b, 0, 1)
            sum_back(b, 1, 1)
            output(b, 1, 1)
            store(b, 1)
